import numpy as np
import ml_dtypes


def mxq(x, axis, fmt="e4m3"):
    dtype, down = {"e4m3": (ml_dtypes.float8_e4m3fn, 7), "e5m2": (ml_dtypes.float8_e5m2, 14)}[fmt]
    v = np.moveaxis(np.asarray(x, np.float32).astype(ml_dtypes.bfloat16).astype(np.float64), axis, -1)
    blocks = v.reshape(v.shape[:-1] + (-1, 32))
    amax = np.abs(blocks).max(-1, keepdims=True)
    byte = np.maximum(np.where(amax > 0, np.frexp(amax)[1] - 1 + 127, 0) - down, 1)
    scale = np.exp2(byte - 127.0)
    codes = (blocks / scale).astype(np.float32).astype(dtype).astype(np.float64)
    return np.moveaxis((codes * scale).reshape(v.shape), -1, axis)


WIDE = False


def mx_kscale(k):
    if not WIDE:
        return np.ones(k)
    levels = np.array([10, -10, 5, -5, 0])
    if k % 512:
        return np.exp2(np.random.permutation(np.resize(levels, k // 32))).repeat(32)
    a = np.empty((k // 512, 16))
    for p in range(k // 512):
        a[p, :8] = np.random.permutation(np.resize(levels, 8))
        for g in range(8):
            far = levels[np.abs(levels - a[p, g]) >= 10]
            a[p, g + 8] = far[np.random.randint(len(far))]
    return np.exp2(a.ravel()).repeat(32)


BF16 = ml_dtypes.bfloat16


def bf(x):
    return np.asarray(x, np.float32).astype(BF16)


def f64(x):
    return np.asarray(x).astype(np.float64)


B, S, DIM, HEADS = 1, 512, 2048, 16
HD = DIM // HEADS
EPS = 1e-6


def rms_norm(x, g):
    var = np.mean(np.square(x), axis=-1, keepdims=True)
    return x * (1.0 / np.sqrt(var + EPS)) * g


def rope(x, cos, sin):
    x1, x2 = np.split(x, 2, axis=-1)
    rot = np.concatenate([-x2, x1], axis=-1)
    return x * cos[None, :, None, :] + rot * sin[None, :, None, :]


def draw0():
    s = mx_kscale(DIM)
    return {
        "hidden_states": bf(np.random.standard_normal((B, S, DIM)) * s),
        "cos": bf(np.random.uniform(-1.0, 1.0, (S, HD))),
        "sin": bf(np.random.uniform(-1.0, 1.0, (S, HD))),
        "w_qk": bf(np.random.standard_normal((DIM + DIM, DIM)) / np.sqrt(DIM) / s[None, :]),
        "b_qk": bf(np.random.standard_normal(DIM + DIM) * 0.2),
        "g_q": bf(1.0 + 0.1 * np.random.standard_normal(DIM)),
        "g_k": bf(1.0 + 0.1 * np.random.standard_normal(DIM)),
    }


def core(hidden_states, cos, sin, w_qk, b_qk, g_q, g_k):
    c, sn = f64(cos), f64(sin)
    qk = (mxq(f64(hidden_states), 2, "e4m3") @ mxq(f64(w_qk), 1, "e4m3").T) + f64(b_qk)
    q = rms_norm(qk[:, :, :DIM], f64(g_q)).reshape(B, S, HEADS, HD)
    k = rms_norm(qk[:, :, DIM:], f64(g_k)).reshape(B, S, HEADS, HD)
    return rope(q, c, sn), rope(k, c, sn)


def e4m3fn_bytes(y):
    return np.clip(np.asarray(y, np.float64), -448.0, 448.0).astype(np.float32).astype(ml_dtypes.float8_e4m3fn).view(np.uint8)


def e4m3fn_values(b):
    return np.asarray(b, np.uint8).view(ml_dtypes.float8_e4m3fn).astype(np.float64)


def setup_inputs():
    d = draw0()
    x0 = np.asarray(d['w_qk']).astype(np.float64)
    s = (np.max(np.abs(x0), axis=(0,), keepdims=True) / 448.0).astype(np.float32)
    out = {}
    for k, v in d.items():
        if k == 'w_qk':
            out['w_qk_bytes'] = e4m3fn_bytes(x0 / s.astype(np.float64))
            out['w_qk_scale'] = s
        else:
            out[k] = v
    return out


def reference(hidden_states, cos, sin, w_qk_bytes, w_qk_scale, b_qk, g_q, g_k):
    return core(hidden_states, cos, sin, e4m3fn_values(w_qk_bytes) * w_qk_scale.astype(np.float64), b_qk, g_q, g_k)

@@ -1,0 +1,374 @@
+from contextlib import ExitStack
+
+import concourse.mybir as mybir
+from concourse.masks import make_identity
+
+F32 = mybir.dt.float32
+BF16 = mybir.dt.bfloat16
+U32 = mybir.dt.uint32
+U8 = mybir.dt.uint8
+FP8 = mybir.dt.float8_e4m3fn
+FP8X4 = mybir.dt.float8_e4m3fn_x4
+ALU = mybir.AluOpType
+ACT = mybir.ActivationFunctionType
+
+P = 128
+S = 512
+DIM = 2048
+HD = 128
+NH = 32
+NPAIR = NH // 2
+PASSES = 4
+TT = 4
+EPS = 1e-6
+FLOPS = 2 * S * 2 * DIM * DIM
+
+
+def tile_dynamicselfattention_pa_kernel(
+    tc, hidden_states, cos, sin, w_qk_bytes, w_qk_scale, b_qk, g_q, g_k, out_0, out_1
+):
+    nc = tc.nc
+    outs = (out_0, out_1)
+    with ExitStack() as ctx:
+        const = ctx.enter_context(tc.tile_pool(name="const", bufs=1))
+        big = ctx.enter_context(tc.tile_pool(name="big", bufs=1))
+        wbp = ctx.enter_context(tc.tile_pool(name="wbp", bufs=2))
+        work = ctx.enter_context(tc.tile_pool(name="work", bufs=2))
+        sqp = ctx.enter_context(tc.tile_pool(name="sqp", bufs=10))
+        prod = ctx.enter_context(tc.tile_pool(name="prod", bufs=2))
+        obp = ctx.enter_context(tc.tile_pool(name="obp", bufs=2))
+        psum = ctx.enter_context(tc.psum_pool(name="psum", bufs=7))
+        psum1 = ctx.enter_context(tc.psum_pool(name="psum1", bufs=1))
+
+        scale2 = const.tile([P, 2 * DIM], F32, name="scale2")
+        w_view = w_qk_bytes.rearrange("(c a p) k -> c p a k", a=2, p=P)
+        wb_tiles = {}
+
+        def load_w(c):
+            wbytes = wbp.tile([P, 2, DIM], U8, name="wbytes")
+            nc.sync.dma_start(out=wbytes[:], in_=w_view[c])
+            wb_tiles[c] = wbytes
+
+        wb_tiles[0] = wbp.tile([P, 2, DIM], U8, name="wbytes")
+        nc.sync.dma_start(out=wb_tiles[0][:, 0, :], in_=w_view[0][:, 0, :])
+        s_rows = const.tile([P, P], F32, name="s_rows")
+        nc.gpsimd.memset(s_rows[:], 0.0)
+        nc.scalar.dma_start(
+            out=s_rows[0:16, :], in_=w_qk_scale.rearrange("o (c p) -> (o c) p", p=P)
+        )
+        nc.sync.dma_start(out=wb_tiles[0][:, 1, :], in_=w_view[0][:, 1, :])
+        load_w(1)
+        hs_view = hidden_states.rearrange("o (j p) k -> (o j) p k", p=P)
+
+        vecs = const.tile([P, P], BF16, name="vecs")
+        nc.gpsimd.memset(vecs[:], 0.0)
+        nc.scalar.dma_start(out=vecs[0:32, :], in_=b_qk.rearrange("(h d) -> h d", d=HD))
+        nc.scalar.dma_start(out=vecs[32:48, :], in_=g_q.rearrange("(h d) -> h d", d=HD))
+        nc.scalar.dma_start(out=vecs[48:64, :], in_=g_k.rearrange("(h d) -> h d", d=HD))
+        cos_t = const.tile([P, TT, HD], BF16, name="cos_t")
+        sin_t = const.tile([P, TT, HD], BF16, name="sin_t")
+        nc.scalar.dma_start(out=cos_t[:], in_=cos.rearrange("(j p) d -> p j d", p=P))
+        nc.scalar.dma_start(out=sin_t[:], in_=sin.rearrange("(j p) d -> p j d", p=P))
+
+        ident = const.tile([P, P], F32, name="ident")
+        make_identity(nc, ident[:])
+        ident_bf = const.tile([P, P], BF16, name="ident_bf")
+        make_identity(nc, ident_bf[:])
+        perm = const.tile([P, P], F32, name="perm")
+        nc.gpsimd.tensor_copy(out=perm[:, 0:64], in_=ident[:, 64:128])
+        nc.gpsimd.tensor_copy(out=perm[:, 64:128], in_=ident[:, 0:64])
+
+        sp = psum.tile([P, P], F32, name="sp", tag="bank")
+        nc.tensor.transpose(sp[:], s_rows[:], ident[:])
+        s_col = const.tile([P, 16], F32, name="s_col")
+        nc.scalar.copy(out=s_col[:], in_=sp[:, 0:16])
+        for b in range(4):
+            sbc = psum.tile([P, 512], F32, name="sbc", tag="bank")
+            for c in range(4):
+                nc.tensor.transpose(
+                    sbc[:, c * P : (c + 1) * P],
+                    s_col[:, 4 * b + c : 4 * b + c + 1].to_broadcast([P, P]),
+                    ident[:],
+                )
+            nc.scalar.copy(out=scale2[:, b * 512 : (b + 1) * 512], in_=sbc[:])
+        nc.scalar.copy(out=scale2[:, DIM : 2 * DIM], in_=scale2[:, 0:DIM])
+
+        hgr = big.tile([P, PASSES * S * 4], BF16, name="hgr", offset=0, align_bytes=64)
+        hgr_w = hgr[:].bitcast(F32).rearrange("p (g s u) -> p g s u", g=PASSES, u=2)
+        hs_codes = const.tile([P, PASSES * S], U32, name="hs_codes", align_bytes=64)
+        hs_sc = const.tile([P, PASSES * S], U8, name="hs_sc", align_bytes=64)
+        for j in range(TT):
+            hs_t = big.tile(
+                [P, DIM], BF16, name="hs_t%d" % j, offset=16384 + 4096 * j, align_bytes=64
+            )
+            nc.sync.dma_start(out=hs_t[:], in_=hs_view[j])
+            words = hs_t[:].bitcast(F32)
+            for b in range(2):
+                xt = psum.tile([P, 512], F32, name="xt", tag="bank")
+                for gg in range(2):
+                    for u in range(2):
+                        g = 2 * b + gg
+                        c0 = (gg * 2 + u) * P
+                        nc.tensor.transpose(
+                            xt[:, c0 : c0 + P], words[:, 256 * g + u : 256 * (g + 1) : 2], ident[:]
+                        )
+                nc.scalar.copy(
+                    out=hgr_w[:, 2 * b : 2 * b + 2, j * P : (j + 1) * P, :],
+                    in_=xt[:].rearrange("p (g u n) -> p g n u", g=2, u=2),
+                )
+
+        vt = psum.tile([P, P], BF16, name="vt", tag="bank")
+        nc.tensor.transpose(vt[:], vecs[:], ident_bf[:])
+        bcol = const.tile([P, NH], F32, name="bcol")
+        gcol = const.tile([P, NH], F32, name="gcol")
+        bgcol = const.tile([P, NH], F32, name="bgcol")
+        nc.scalar.copy(out=bcol[:], in_=vt[:, 0:32])
+        nc.scalar.copy(out=gcol[:], in_=vt[:, 32:64])
+
+        cosT4 = const.tile([P, 4, S], BF16, name="cosT4")
+        sinT4 = const.tile([P, 4, S], BF16, name="sinT4")
+
+        def rope_tables():
+            sinsw = const.tile([P, TT, HD], BF16, name="sinsw")
+            nc.vector.tensor_copy(out=sinsw[:, :, 0:64], in_=sin_t[:, :, 64:128])
+            nc.vector.tensor_scalar(
+                out=sinsw[:, :, 64:128],
+                in0=sin_t[:, :, 0:64],
+                scalar1=-1.0,
+                scalar2=None,
+                op0=ALU.mult,
+            )
+            for src_t, dst_t in ((cos_t, cosT4), (sinsw, sinT4)):
+                tb = psum.tile([P, S], BF16, name="tb", tag="bank")
+                for j in range(TT):
+                    nc.tensor.transpose(tb[:, j * P : (j + 1) * P], src_t[:, j, :], ident_bf[:])
+                for c in range(4):
+                    nc.scalar.copy(out=dst_t[:, c, :], in_=tb[:])
+
+        def quantize_hidden():
+            for c in range(2):
+                nc.vector.quantize_mx(
+                    out=hs_codes[:, c * 1024 : (c + 1) * 1024].bitcast(FP8X4),
+                    scales=hs_sc[:, c * 1024 : (c + 1) * 1024],
+                    in_=hgr[:, c * 4096 : (c + 1) * 4096],
+                )
+
+        y_all = big.tile([P, NH, S], F32, name="y_all", offset=0, align_bytes=64)
+        part = const.tile([P, 16], F32, name="part")
+        rstd = [const.tile([P, TT], F32, name="rstd%d" % i) for i in range(2)]
+        st = {}
+
+        def widen(ip):
+            wide = work.tile([P, 2 * DIM], BF16, name="wide")
+            wb = wb_tiles[ip][:].rearrange("p a k -> p (a k)")
+            bounds = (0, 512, 1024, 1536, 2048, 4096) if ip == 0 else (0, 4096)
+            for lo, hi in zip(bounds[:-1], bounds[1:]):
+                sc_lo = lo % DIM if ip == 0 else lo
+                nc.vector.tensor_tensor(
+                    out=wide[:, lo:hi],
+                    in0=wb[:, lo:hi].bitcast(FP8),
+                    in1=scale2[:, sc_lo : sc_lo + hi - lo],
+                    op=ALU.mult,
+                )
+            st[("wide", ip)] = wide
+
+        def turn(ip):
+            words = st[("wide", ip)][:].bitcast(F32)
+            sorted_w = work.tile([P, DIM // 2], F32, name="sorted_w")
+            nc.scalar.copy(
+                out=sorted_w[:].rearrange("p (g u q) -> p g u q", g=PASSES, u=2),
+                in_=words[:, DIM // 2 : DIM].rearrange("p (g q u) -> p g u q", g=PASSES, u=2),
+            )
+            grouped = work.tile([P, 2 * DIM], BF16, name="grouped", align_bytes=64)
+            gw = grouped[:].bitcast(F32).rearrange("p (b g n u) -> p b g n u", b=4, g=2, u=2)
+            for b in range(4):
+                xt = psum.tile([P, 512], F32, name="xt", tag="bank")
+                for gg in range(2):
+                    for u in range(2):
+                        w0 = 256 * (2 * b + gg)
+                        c0 = (gg * 2 + u) * P
+                        s0 = w0 - DIM // 2 + u * P
+                        nc.tensor.transpose(
+                            xt[:, c0 : c0 + P],
+                            words[:, w0 + u : w0 + 256 : 2] if b < 2 else sorted_w[:, s0 : s0 + P],
+                            ident[:],
+                        )
+                nc.scalar.copy(
+                    out=gw[:, b, :, :, :], in_=xt[:].rearrange("p (g u n) -> p g n u", g=2, u=2)
+                )
+            st[("grouped", ip)] = grouped
+
+        def project(ip):
+            codes = work.tile([P, 2 * PASSES * P], U32, name="codes", align_bytes=64)
+            wsc = work.tile([P, 2 * PASSES * P], U8, name="wsc", align_bytes=64)
+            nc.vector.quantize_mx(
+                out=codes[:].bitcast(FP8X4), scales=wsc[:], in_=st[("grouped", ip)][:]
+            )
+            accs = []
+            for a in range(2):
+                acc = psum.tile([P, S], F32, name="acc", tag="bank")
+                accs.append(acc)
+                for g in range(PASSES):
+                    cols = slice((a * PASSES + g) * P, (a * PASSES + g + 1) * P)
+                    nc.tensor.matmul_mx(
+                        out=acc[:],
+                        lhsT=codes[:, cols].bitcast(FP8X4),
+                        lhsT_scale=wsc[:, cols],
+                        rhs=hs_codes[:, g * S : (g + 1) * S].bitcast(FP8X4),
+                        rhs_scale=hs_sc[:, g * S : (g + 1) * S],
+                        start=(g == 0),
+                        stop=(g == PASSES - 1),
+                    )
+            for a in range(2):
+                h = 2 * ip + a
+                nc.scalar.activation(
+                    out=y_all[:, h, :],
+                    in_=accs[a][:],
+                    func=ACT.Identity,
+                    bias=bgcol[:, h : h + 1],
+                    scale=gcol[:, h : h + 1],
+                )
+                sq = sqp.tile([P, S], F32, name="sq")
+                nc.scalar.activation(
+                    out=sq[:], in_=accs[a][:], func=ACT.Square, bias=bcol[:, h : h + 1], scale=1.0
+                )
+                st[("sq", h)] = sq
+
+        def sumsq(r):
+            ssb = psum1.tile([P, TT, HD], F32, name="ssb")
+            for j in range(TT):
+                for hh in range(8):
+                    nc.tensor.matmul(
+                        out=ssb[:, j, :],
+                        lhsT=st[("sq", 8 * r + hh)][:, j * P : (j + 1) * P],
+                        rhs=ident[:],
+                        start=(hh == 0),
+                        stop=(hh == 7),
+                        is_transpose=True,
+                    )
+            for j in range(TT):
+                junk = work.tile([P, HD], F32, name="junk")
+                nc.scalar.activation(
+                    out=junk[:],
+                    in_=ssb[:, j, :],
+                    func=ACT.Copy,
+                    accum_out=part[:, 4 * r + j : 4 * r + j + 1],
+                )
+
+        def norm_a(qk):
+            ssum = work.tile([P, TT], F32, name="ssum")
+            nc.vector.tensor_tensor(
+                out=ssum[:],
+                in0=part[:, 8 * qk : 8 * qk + 4],
+                in1=part[:, 8 * qk + 4 : 8 * qk + 8],
+                op=ALU.add,
+            )
+            ms = work.tile([P, TT], F32, name="ms")
+            nc.vector.tensor_scalar(
+                out=ms[:], in0=ssum[:], scalar1=1.0 / DIM, scalar2=EPS, op0=ALU.mult, op1=ALU.add
+            )
+            rms = work.tile([P, TT], F32, name="rms")
+            nc.scalar.activation(out=rms[:], in_=ms[:], func=ACT.Sqrt)
+            st[("rms", qk)] = rms
+
+        def norm_b(qk):
+            nc.vector.reciprocal(out=rstd[qk][:], in_=st[("rms", qk)][:])
+
+        def products(h0, n):
+            a_c = prod.tile([P, 4, S], F32, name="a_c")
+            z_c = prod.tile([P, 4, S], F32, name="z_c")
+            nc.vector.tensor_tensor(
+                out=a_c[:, 0:n, :], in0=y_all[:, h0 : h0 + n, :], in1=cosT4[:, 0:n, :], op=ALU.mult
+            )
+            nc.vector.tensor_tensor(
+                out=z_c[:, 0:n, :], in0=y_all[:, h0 : h0 + n, :], in1=sinT4[:, 0:n, :], op=ALU.mult
+            )
+            st[("a", h0)] = a_c
+            st[("z", h0)] = z_c
+
+        def back(h0, n):
+            a_c = st[("a", h0)]
+            z_c = st[("z", h0)]
+            for j in range(TT):
+                ob = psum.tile([P, 4, HD], F32, name="ob", tag="bank")
+                st[("ob", h0, j)] = ob
+                for hh in range(n):
+                    nc.tensor.matmul(
+                        out=ob[:, hh, :],
+                        lhsT=a_c[:, hh, j * P : (j + 1) * P],
+                        rhs=ident[:],
+                        start=True,
+                        stop=False,
+                        is_transpose=True,
+                    )
+                    nc.tensor.matmul(
+                        out=ob[:, hh, :],
+                        lhsT=z_c[:, hh, j * P : (j + 1) * P],
+                        rhs=perm[:],
+                        start=False,
+                        stop=True,
+                        is_transpose=True,
+                    )
+
+        def emit(h0, n):
+            qk = h0 // 16
+            obuf = obp.tile([P, TT, 4, HD], F32, name="obuf")
+            for j in range(TT):
+                nc.scalar.activation(
+                    out=obuf[:, j, 0:n, :],
+                    in_=st[("ob", h0, j)][:, 0:n, :],
+                    func=ACT.Copy,
+                    scale=rstd[qk][:, j : j + 1],
+                )
+            c0 = (h0 % 16) * HD
+            dst = outs[qk].rearrange("o (j p) h d -> p (o j) (h d)", p=P)
+            nc.sync.dma_start(
+                out=dst[:, :, c0 : c0 + n * HD],
+                in_=obuf[:, :, 0:n, :].rearrange("p j h d -> p j (h d)"),
+            )
+
+        Q_ROPE = {12: 0, 14: 4, 16: 8, 17: 12}
+        for ip in range(NPAIR + 2):
+            if ip < NPAIR:
+                widen(ip)
+                if ip + 2 < NPAIR:
+                    load_w(ip + 2)
+            if ip == 2:
+                nc.vector.tensor_tensor(out=bgcol[:], in0=bcol[:], in1=gcol[:], op=ALU.mult)
+                quantize_hidden()
+            if ip == 3:
+                rope_tables()
+            if 0 <= ip - 1 < NPAIR:
+                turn(ip - 1)
+            if ip in (6, 10, 14):
+                sumsq((ip - 6) // 4)
+            if ip in Q_ROPE and ip >= NPAIR:
+                products(Q_ROPE[ip], 4)
+            if 0 <= ip - 2 < NPAIR:
+                project(ip - 2)
+            if ip == 10:
+                norm_a(0)
+            if ip == 11:
+                norm_b(0)
+            if ip in Q_ROPE:
+                if ip < NPAIR:
+                    products(Q_ROPE[ip], 4)
+                back(Q_ROPE[ip], 4)
+                emit(Q_ROPE[ip], 4)
+        sumsq(3)
+        groups = ((16, 4), (20, 4), (24, 4), (28, 2), (30, 1), (31, 1))
+        products(16, 4)
+        products(20, 4)
+        back(16, 4)
+        norm_a(1)
+        products(24, 4)
+        norm_b(1)
+        emit(16, 4)
+        back(20, 4)
+        for i in range(3, len(groups)):
+            products(groups[i][0], groups[i][1])
+            emit(groups[i - 2][0], groups[i - 2][1])
+            back(groups[i - 1][0], groups[i - 1][1])
+        emit(30, 1)
+        back(31, 1)
+        emit(31, 1)

@@ -36,7 +36,7 @@ def tile_dynamicselfattention_pa_kernel(
         work = ctx.enter_context(tc.tile_pool(name="work", bufs=2))
         sqp = ctx.enter_context(tc.tile_pool(name="sqp", bufs=10))
         prod = ctx.enter_context(tc.tile_pool(name="prod", bufs=2))
-        obp = ctx.enter_context(tc.tile_pool(name="obp", bufs=2))
+        obp = ctx.enter_context(tc.tile_pool(name="obp", bufs=8))
         psum = ctx.enter_context(tc.psum_pool(name="psum", bufs=7))
         psum1 = ctx.enter_context(tc.psum_pool(name="psum1", bufs=1))
 
@@ -312,20 +312,20 @@ def tile_dynamicselfattention_pa_kernel(
 
         def emit(h0, n):
             qk = h0 // 16
-            obuf = obp.tile([P, TT, 4, HD], F32, name="obuf")
+            c0 = (h0 % 16) * HD
+            dst = outs[qk].rearrange("o (j p) h d -> p (o j) (h d)", p=P)
             for j in range(TT):
+                obuf = obp.tile([P, 4, HD], F32, name="obuf")
                 nc.scalar.activation(
-                    out=obuf[:, j, 0:n, :],
+                    out=obuf[:, 0:n, :],
                     in_=st[("ob", h0, j)][:, 0:n, :],
                     func=ACT.Copy,
                     scale=rstd[qk][:, j : j + 1],
                 )
-            c0 = (h0 % 16) * HD
-            dst = outs[qk].rearrange("o (j p) h d -> p (o j) (h d)", p=P)
-            nc.sync.dma_start(
-                out=dst[:, :, c0 : c0 + n * HD],
-                in_=obuf[:, :, 0:n, :].rearrange("p j h d -> p j (h d)"),
-            )
+                nc.sync.dma_start(
+                    out=dst[:, j, c0 : c0 + n * HD],
+                    in_=obuf[:, 0:n, :].rearrange("p h d -> p (h d)"),
+                )
 
         Q_ROPE = {12: 0, 14: 4, 16: 8, 17: 12}
         for ip in range(NPAIR + 2):

@@ -21,6 +21,7 @@ NPAIR = NH // 2
 PASSES = 4
 TT = 4
 EPS = 1e-6
+V_CAST = 1024
 FLOPS = 2 * S * 2 * DIM * DIM
 
 
@@ -32,15 +33,15 @@ def tile_dynamicselfattention_pa_kernel(
     with ExitStack() as ctx:
         const = ctx.enter_context(tc.tile_pool(name="const", bufs=1))
         big = ctx.enter_context(tc.tile_pool(name="big", bufs=1))
-        wbp = ctx.enter_context(tc.tile_pool(name="wbp", bufs=2))
+        wbp = ctx.enter_context(tc.tile_pool(name="wbp", bufs=3))
+        widep = ctx.enter_context(tc.tile_pool(name="widep", bufs=3))
         work = ctx.enter_context(tc.tile_pool(name="work", bufs=2))
         sqp = ctx.enter_context(tc.tile_pool(name="sqp", bufs=10))
-        prod = ctx.enter_context(tc.tile_pool(name="prod", bufs=2))
+        zp = ctx.enter_context(tc.tile_pool(name="zp", bufs=10))
         obp = ctx.enter_context(tc.tile_pool(name="obp", bufs=8))
         psum = ctx.enter_context(tc.psum_pool(name="psum", bufs=7))
         psum1 = ctx.enter_context(tc.psum_pool(name="psum1", bufs=1))
 
-        scale2 = const.tile([P, 2 * DIM], F32, name="scale2")
         w_view = w_qk_bytes.rearrange("(c a p) k -> c p a k", a=2, p=P)
         wb_tiles = {}
 
@@ -51,14 +52,22 @@ def tile_dynamicselfattention_pa_kernel(
 
         wb_tiles[0] = wbp.tile([P, 2, DIM], U8, name="wbytes")
         nc.sync.dma_start(out=wb_tiles[0][:, 0, :], in_=w_view[0][:, 0, :])
-        s_rows = const.tile([P, P], F32, name="s_rows")
-        nc.gpsimd.memset(s_rows[:], 0.0)
-        nc.scalar.dma_start(
-            out=s_rows[0:16, :], in_=w_qk_scale.rearrange("o (c p) -> (o c) p", p=P)
-        )
         nc.sync.dma_start(out=wb_tiles[0][:, 1, :], in_=w_view[0][:, 1, :])
-        load_w(1)
+        scale_t = const.tile([P, PASSES, 1, 4], F32, name="scale_t")
+        nc.scalar.dma_start(
+            out=scale_t[:].rearrange("p g o t -> p (g o) t"),
+            in_=w_qk_scale.rearrange("o (g p t) -> p (o g) t", p=P, t=4),
+        )
         hs_view = hidden_states.rearrange("o (j p) k -> (o j) p k", p=P)
+        hs_tiles = []
+        for j in range(TT):
+            hs_t = big.tile(
+                [P, DIM], BF16, name="hs_t%d" % j, offset=16384 + 4096 * j, align_bytes=64
+            )
+            nc.sync.dma_start(out=hs_t[:], in_=hs_view[j])
+            hs_tiles.append(hs_t)
+        load_w(1)
+        load_w(2)
 
         vecs = const.tile([P, P], BF16, name="vecs")
         nc.gpsimd.memset(vecs[:], 0.0)
@@ -78,72 +87,29 @@ def tile_dynamicselfattention_pa_kernel(
         nc.gpsimd.tensor_copy(out=perm[:, 0:64], in_=ident[:, 64:128])
         nc.gpsimd.tensor_copy(out=perm[:, 64:128], in_=ident[:, 0:64])
 
-        sp = psum.tile([P, P], F32, name="sp", tag="bank")
-        nc.tensor.transpose(sp[:], s_rows[:], ident[:])
-        s_col = const.tile([P, 16], F32, name="s_col")
-        nc.scalar.copy(out=s_col[:], in_=sp[:, 0:16])
-        for b in range(4):
-            sbc = psum.tile([P, 512], F32, name="sbc", tag="bank")
-            for c in range(4):
-                nc.tensor.transpose(
-                    sbc[:, c * P : (c + 1) * P],
-                    s_col[:, 4 * b + c : 4 * b + c + 1].to_broadcast([P, P]),
-                    ident[:],
-                )
-            nc.scalar.copy(out=scale2[:, b * 512 : (b + 1) * 512], in_=sbc[:])
-        nc.scalar.copy(out=scale2[:, DIM : 2 * DIM], in_=scale2[:, 0:DIM])
-
         hgr = big.tile([P, PASSES * S * 4], BF16, name="hgr", offset=0, align_bytes=64)
         hgr_w = hgr[:].bitcast(F32).rearrange("p (g s u) -> p g s u", g=PASSES, u=2)
         hs_codes = const.tile([P, PASSES * S], U32, name="hs_codes", align_bytes=64)
         hs_sc = const.tile([P, PASSES * S], U8, name="hs_sc", align_bytes=64)
-        for j in range(TT):
-            hs_t = big.tile(
-                [P, DIM], BF16, name="hs_t%d" % j, offset=16384 + 4096 * j, align_bytes=64
-            )
-            nc.sync.dma_start(out=hs_t[:], in_=hs_view[j])
-            words = hs_t[:].bitcast(F32)
-            for b in range(2):
-                xt = psum.tile([P, 512], F32, name="xt", tag="bank")
-                for gg in range(2):
-                    for u in range(2):
-                        g = 2 * b + gg
-                        c0 = (gg * 2 + u) * P
-                        nc.tensor.transpose(
-                            xt[:, c0 : c0 + P], words[:, 256 * g + u : 256 * (g + 1) : 2], ident[:]
-                        )
-                nc.scalar.copy(
-                    out=hgr_w[:, 2 * b : 2 * b + 2, j * P : (j + 1) * P, :],
-                    in_=xt[:].rearrange("p (g u n) -> p g n u", g=2, u=2),
-                )
 
-        vt = psum.tile([P, P], BF16, name="vt", tag="bank")
-        nc.tensor.transpose(vt[:], vecs[:], ident_bf[:])
-        bcol = const.tile([P, NH], F32, name="bcol")
-        gcol = const.tile([P, NH], F32, name="gcol")
-        bgcol = const.tile([P, NH], F32, name="bgcol")
-        nc.scalar.copy(out=bcol[:], in_=vt[:, 0:32])
-        nc.scalar.copy(out=gcol[:], in_=vt[:, 32:64])
-
-        cosT4 = const.tile([P, 4, S], BF16, name="cosT4")
-        sinT4 = const.tile([P, 4, S], BF16, name="sinT4")
-
-        def rope_tables():
-            sinsw = const.tile([P, TT, HD], BF16, name="sinsw")
-            nc.vector.tensor_copy(out=sinsw[:, :, 0:64], in_=sin_t[:, :, 64:128])
-            nc.vector.tensor_scalar(
-                out=sinsw[:, :, 64:128],
-                in0=sin_t[:, :, 0:64],
-                scalar1=-1.0,
-                scalar2=None,
-                op0=ALU.mult,
-            )
-            for src_t, dst_t in ((cos_t, cosT4), (sinsw, sinT4)):
-                tb = psum.tile([P, S], BF16, name="tb", tag="bank")
-                for j in range(TT):
-                    nc.tensor.transpose(tb[:, j * P : (j + 1) * P], src_t[:, j, :], ident_bf[:])
-                for c in range(4):
-                    nc.scalar.copy(out=dst_t[:, c, :], in_=tb[:])
+        def turn_hidden():
+            for j in range(TT):
+                words = hs_tiles[j][:].bitcast(F32)
+                for b in range(2):
+                    xt = psum.tile([P, 512], F32, name="xt", tag="bank")
+                    for gg in range(2):
+                        for u in range(2):
+                            g = 2 * b + gg
+                            c0 = (gg * 2 + u) * P
+                            nc.tensor.transpose(
+                                xt[:, c0 : c0 + P],
+                                words[:, 256 * g + u : 256 * (g + 1) : 2],
+                                ident[:],
+                            )
+                    nc.scalar.copy(
+                        out=hgr_w[:, 2 * b : 2 * b + 2, j * P : (j + 1) * P, :],
+                        in_=xt[:].rearrange("p (g u n) -> p g n u", g=2, u=2),
+                    )
 
         def quantize_hidden():
             for c in range(2):
@@ -153,63 +119,103 @@ def tile_dynamicselfattention_pa_kernel(
                     in_=hgr[:, c * 4096 : (c + 1) * 4096],
                 )
 
+        bcol = const.tile([P, NH], F32, name="bcol")
+        gcol = const.tile([P, NH], F32, name="gcol")
+        bgcol = const.tile([P, NH], F32, name="bgcol")
+
+        def columns():
+            vt = psum.tile([P, P], BF16, name="vt", tag="bank")
+            nc.tensor.transpose(vt[:], vecs[:], ident_bf[:])
+            nc.scalar.copy(out=bcol[:], in_=vt[:, 0:32])
+            nc.scalar.copy(out=gcol[:], in_=vt[:, 32:64])
+            nc.gpsimd.tensor_tensor(out=bgcol[:], in0=bcol[:], in1=gcol[:], op=ALU.mult)
+
+        cosT = const.tile([P, 1, S], BF16, name="cosT")
+        sinT = const.tile([P, 1, S], BF16, name="sinT")
+
+        def rope_tables():
+            sinsw = const.tile([P, TT, HD], BF16, name="sinsw")
+            nc.gpsimd.tensor_copy(out=sinsw[:, :, 0:64], in_=sin_t[:, :, 64:128])
+            nc.gpsimd.tensor_scalar(
+                out=sinsw[:, :, 64:128],
+                in0=sin_t[:, :, 0:64],
+                scalar1=-1.0,
+                scalar2=0.0,
+                op0=ALU.mult,
+                op1=ALU.add,
+            )
+            for src_t, dst_t in ((cos_t, cosT), (sinsw, sinT)):
+                tb = psum.tile([P, S], BF16, name="tb", tag="bank")
+                for j in range(TT):
+                    nc.tensor.transpose(tb[:, j * P : (j + 1) * P], src_t[:, j, :], ident_bf[:])
+                nc.scalar.copy(out=dst_t[:, 0, :], in_=tb[:])
+
         y_all = big.tile([P, NH, S], F32, name="y_all", offset=0, align_bytes=64)
-        part = const.tile([P, 16], F32, name="part")
+        part = const.tile([P, 5, TT], F32, name="part")
         rstd = [const.tile([P, TT], F32, name="rstd%d" % i) for i in range(2)]
         st = {}
 
-        def widen(ip):
-            wide = work.tile([P, 2 * DIM], BF16, name="wide")
+        def cast(ip):
+            wide = widep.tile([P, 2 * DIM], BF16, name="wide")
             wb = wb_tiles[ip][:].rearrange("p a k -> p (a k)")
-            bounds = (0, 512, 1024, 1536, 2048, 4096) if ip == 0 else (0, 4096)
-            for lo, hi in zip(bounds[:-1], bounds[1:]):
-                sc_lo = lo % DIM if ip == 0 else lo
-                nc.vector.tensor_tensor(
-                    out=wide[:, lo:hi],
-                    in0=wb[:, lo:hi].bitcast(FP8),
-                    in1=scale2[:, sc_lo : sc_lo + hi - lo],
-                    op=ALU.mult,
+            if ip == 0:
+                shares = ((0, DIM, nc.vector.tensor_copy), (DIM, 2 * DIM, nc.scalar.copy))
+            elif ip <= 2:
+                shares = (
+                    (0, DIM, nc.gpsimd.tensor_copy),
+                    (DIM, 2 * DIM, nc.gpsimd.tensor_copy),
                 )
+            else:
+                shares = (
+                    (0, V_CAST, nc.vector.tensor_copy),
+                    (V_CAST, DIM, nc.scalar.copy),
+                    (DIM, 2 * DIM, nc.scalar.copy),
+                )
+            for lo, hi, copy in shares:
+                copy(out=wide[:, lo:hi], in_=wb[:, lo:hi].bitcast(FP8))
             st[("wide", ip)] = wide
 
         def turn(ip):
             words = st[("wide", ip)][:].bitcast(F32)
-            sorted_w = work.tile([P, DIM // 2], F32, name="sorted_w")
-            nc.scalar.copy(
-                out=sorted_w[:].rearrange("p (g u q) -> p g u q", g=PASSES, u=2),
-                in_=words[:, DIM // 2 : DIM].rearrange("p (g q u) -> p g u q", g=PASSES, u=2),
-            )
             grouped = work.tile([P, 2 * DIM], BF16, name="grouped", align_bytes=64)
-            gw = grouped[:].bitcast(F32).rearrange("p (b g n u) -> p b g n u", b=4, g=2, u=2)
-            for b in range(4):
-                xt = psum.tile([P, 512], F32, name="xt", tag="bank")
-                for gg in range(2):
+            gv = grouped[:].rearrange("p (g m u e) -> p g m u e", g=PASSES, u=2, e=2)
+            for g in range(PASSES):
+                xt = psum.tile([P, 2, 2, P], F32, name="xt", tag="bank")
+                for a in range(2):
                     for u in range(2):
-                        w0 = 256 * (2 * b + gg)
-                        c0 = (gg * 2 + u) * P
-                        s0 = w0 - DIM // 2 + u * P
+                        w0 = a * (DIM // 2) + 256 * g
                         nc.tensor.transpose(
-                            xt[:, c0 : c0 + P],
-                            words[:, w0 + u : w0 + 256 : 2] if b < 2 else sorted_w[:, s0 : s0 + P],
-                            ident[:],
+                            xt[:, u, a, :], words[:, w0 + u : w0 + 256 : 2], ident[:]
                         )
-                nc.scalar.copy(
-                    out=gw[:, b, :, :, :], in_=xt[:].rearrange("p (g u n) -> p g n u", g=2, u=2)
+                nc.vector.tensor_tensor(
+                    out=gv[:, g, :, :, :],
+                    in0=xt[:]
+                    .rearrange("p u a n -> p u (a n)")
+                    .bitcast(BF16)
+                    .rearrange("p u (m e) -> p m u e", e=2),
+                    in1=scale_t[:, g, :, :]
+                    .to_broadcast([P, 2 * P, 4])
+                    .rearrange("p m (u e) -> p m u e", e=2),
+                    op=ALU.mult,
                 )
             st[("grouped", ip)] = grouped
 
-        def project(ip):
+        def quantize(ip):
             codes = work.tile([P, 2 * PASSES * P], U32, name="codes", align_bytes=64)
             wsc = work.tile([P, 2 * PASSES * P], U8, name="wsc", align_bytes=64)
             nc.vector.quantize_mx(
                 out=codes[:].bitcast(FP8X4), scales=wsc[:], in_=st[("grouped", ip)][:]
             )
+            st[("codes", ip)] = (codes, wsc)
+
+        def project(ip):
+            codes, wsc = st[("codes", ip)]
             accs = []
             for a in range(2):
                 acc = psum.tile([P, S], F32, name="acc", tag="bank")
                 accs.append(acc)
                 for g in range(PASSES):
-                    cols = slice((a * PASSES + g) * P, (a * PASSES + g + 1) * P)
+                    cols = slice((2 * g + a) * P, (2 * g + a + 1) * P)
                     nc.tensor.matmul_mx(
                         out=acc[:],
                         lhsT=codes[:, cols].bitcast(FP8X4),
@@ -234,34 +240,30 @@ def tile_dynamicselfattention_pa_kernel(
                 )
                 st[("sq", h)] = sq
 
+        ROUNDS = ((0, 8), (8, 16), (16, 24), (24, 30), (30, 32))
+
         def sumsq(r):
+            lo, hi = ROUNDS[r]
             ssb = psum1.tile([P, TT, HD], F32, name="ssb")
             for j in range(TT):
-                for hh in range(8):
+                for h in range(lo, hi):
                     nc.tensor.matmul(
                         out=ssb[:, j, :],
-                        lhsT=st[("sq", 8 * r + hh)][:, j * P : (j + 1) * P],
+                        lhsT=st[("sq", h)][:, j * P : (j + 1) * P],
                         rhs=ident[:],
-                        start=(hh == 0),
-                        stop=(hh == 7),
+                        start=(h == lo),
+                        stop=(h == hi - 1),
                         is_transpose=True,
                     )
-            for j in range(TT):
-                junk = work.tile([P, HD], F32, name="junk")
-                nc.scalar.activation(
-                    out=junk[:],
-                    in_=ssb[:, j, :],
-                    func=ACT.Copy,
-                    accum_out=part[:, 4 * r + j : 4 * r + j + 1],
-                )
+            nc.vector.reduce_sum(out=part[:, r, :], in_=ssb[:], axis=mybir.AxisListType.X)
 
         def norm_a(qk):
+            rounds = slice(0, 2) if qk == 0 else slice(2, 5)
             ssum = work.tile([P, TT], F32, name="ssum")
-            nc.vector.tensor_tensor(
+            nc.vector.reduce_sum(
                 out=ssum[:],
-                in0=part[:, 8 * qk : 8 * qk + 4],
-                in1=part[:, 8 * qk + 4 : 8 * qk + 8],
-                op=ALU.add,
+                in_=part[:, rounds, :].rearrange("p r j -> p j r"),
+                axis=mybir.AxisListType.X,
             )
             ms = work.tile([P, TT], F32, name="ms")
             nc.vector.tensor_scalar(
@@ -274,28 +276,22 @@ def tile_dynamicselfattention_pa_kernel(
         def norm_b(qk):
             nc.vector.reciprocal(out=rstd[qk][:], in_=st[("rms", qk)][:])
 
-        def products(h0, n):
-            a_c = prod.tile([P, 4, S], F32, name="a_c")
-            z_c = prod.tile([P, 4, S], F32, name="z_c")
-            nc.vector.tensor_tensor(
-                out=a_c[:, 0:n, :], in0=y_all[:, h0 : h0 + n, :], in1=cosT4[:, 0:n, :], op=ALU.mult
-            )
-            nc.vector.tensor_tensor(
-                out=z_c[:, 0:n, :], in0=y_all[:, h0 : h0 + n, :], in1=sinT4[:, 0:n, :], op=ALU.mult
-            )
-            st[("a", h0)] = a_c
-            st[("z", h0)] = z_c
+        def products(ip, eng):
+            y = y_all[:, 2 * ip : 2 * ip + 2, :]
+            z = zp.tile([P, 2, S], F32, name="z")
+            eng.tensor_tensor(out=z[:], in0=y, in1=sinT[:].to_broadcast([P, 2, S]), op=ALU.mult)
+            eng.tensor_tensor(out=y, in0=y, in1=cosT[:].to_broadcast([P, 2, S]), op=ALU.mult)
+            st[("z", ip)] = z
 
         def back(h0, n):
-            a_c = st[("a", h0)]
-            z_c = st[("z", h0)]
             for j in range(TT):
                 ob = psum.tile([P, 4, HD], F32, name="ob", tag="bank")
                 st[("ob", h0, j)] = ob
                 for hh in range(n):
+                    h = h0 + hh
                     nc.tensor.matmul(
                         out=ob[:, hh, :],
-                        lhsT=a_c[:, hh, j * P : (j + 1) * P],
+                        lhsT=y_all[:, h, j * P : (j + 1) * P],
                         rhs=ident[:],
                         start=True,
                         stop=False,
@@ -303,72 +299,99 @@ def tile_dynamicselfattention_pa_kernel(
                     )
                     nc.tensor.matmul(
                         out=ob[:, hh, :],
-                        lhsT=z_c[:, hh, j * P : (j + 1) * P],
+                        lhsT=st[("z", h // 2)][:, h % 2, j * P : (j + 1) * P],
                         rhs=perm[:],
                         start=False,
                         stop=True,
                         is_transpose=True,
                     )
 
-        def emit(h0, n):
+        def emit(h0, n, shared):
             qk = h0 // 16
             c0 = (h0 % 16) * HD
             dst = outs[qk].rearrange("o (j p) h d -> p (o j) (h d)", p=P)
             for j in range(TT):
                 obuf = obp.tile([P, 4, HD], F32, name="obuf")
-                nc.scalar.activation(
-                    out=obuf[:, 0:n, :],
-                    in_=st[("ob", h0, j)][:, 0:n, :],
-                    func=ACT.Copy,
-                    scale=rstd[qk][:, j : j + 1],
-                )
+                ob = st[("ob", h0, j)]
+                if shared and j % 2 == 1:
+                    nc.vector.tensor_scalar(
+                        out=obuf[:, 0:n, :],
+                        in0=ob[:, 0:n, :],
+                        scalar1=rstd[qk][:, j : j + 1],
+                        scalar2=None,
+                        op0=ALU.mult,
+                    )
+                else:
+                    nc.scalar.activation(
+                        out=obuf[:, 0:n, :],
+                        in_=ob[:, 0:n, :],
+                        func=ACT.Copy,
+                        scale=rstd[qk][:, j : j + 1],
+                    )
                 nc.sync.dma_start(
                     out=dst[:, j, c0 : c0 + n * HD],
                     in_=obuf[:, 0:n, :].rearrange("p h d -> p (h d)"),
                 )
 
-        Q_ROPE = {12: 0, 14: 4, 16: 8, 17: 12}
-        for ip in range(NPAIR + 2):
+        def park(h0):
+            for j in range(TT):
+                nc.scalar.copy(
+                    out=y_all[:, h0 - 16 + j, :],
+                    in_=st[("ob", h0, j)][:].rearrange("p h d -> p (h d)"),
+                )
+
+        def emit_parked(h0):
+            c0 = (h0 - 16) * HD
+            dst = outs[1].rearrange("o (j p) h d -> p (o j) (h d)", p=P)
+            for j in range(TT):
+                y = y_all[:, h0 - 16 + j, :]
+                nc.vector.tensor_scalar(
+                    out=y, in0=y, scalar1=rstd[1][:, j : j + 1], scalar2=None, op0=ALU.mult
+                )
+                nc.sync.dma_start(out=dst[:, j, c0 : c0 + 4 * HD], in_=y)
+
+        Q_OUT = {12: 0, 13: 4, 14: 8, 15: 12}
+        K_PARK = {16: 16, 17: 20}
+        for ip in range(NPAIR + 3):
             if ip < NPAIR:
-                widen(ip)
-                if ip + 2 < NPAIR:
-                    load_w(ip + 2)
-            if ip == 2:
-                nc.vector.tensor_tensor(out=bgcol[:], in0=bcol[:], in1=gcol[:], op=ALU.mult)
-                quantize_hidden()
-            if ip == 3:
-                rope_tables()
+                cast(ip)
+                if ip + 3 < NPAIR:
+                    load_w(ip + 3)
+            if 0 <= ip - 2 < NPAIR:
+                quantize(ip - 2)
             if 0 <= ip - 1 < NPAIR:
                 turn(ip - 1)
-            if ip in (6, 10, 14):
-                sumsq((ip - 6) // 4)
-            if ip in Q_ROPE and ip >= NPAIR:
-                products(Q_ROPE[ip], 4)
+            if ip == 1:
+                turn_hidden()
+                quantize_hidden()
+                columns()
+            if ip == 2:
+                rope_tables()
+            if ip in (6, 10, 14, 17):
+                sumsq({6: 0, 10: 1, 14: 2, 17: 3}[ip])
             if 0 <= ip - 2 < NPAIR:
                 project(ip - 2)
+            if 0 <= ip - 3 < NPAIR:
+                products(ip - 3, nc.gpsimd if ip - 3 < NPAIR - 2 else nc.vector)
             if ip == 10:
                 norm_a(0)
             if ip == 11:
                 norm_b(0)
-            if ip in Q_ROPE:
-                if ip < NPAIR:
-                    products(Q_ROPE[ip], 4)
-                back(Q_ROPE[ip], 4)
-                emit(Q_ROPE[ip], 4)
-        sumsq(3)
-        groups = ((16, 4), (20, 4), (24, 4), (28, 2), (30, 1), (31, 1))
-        products(16, 4)
-        products(20, 4)
-        back(16, 4)
-        norm_a(1)
-        products(24, 4)
-        norm_b(1)
-        emit(16, 4)
-        back(20, 4)
-        for i in range(3, len(groups)):
-            products(groups[i][0], groups[i][1])
-            emit(groups[i - 2][0], groups[i - 2][1])
-            back(groups[i - 1][0], groups[i - 1][1])
-        emit(30, 1)
-        back(31, 1)
-        emit(31, 1)
+            if ip in Q_OUT:
+                back(Q_OUT[ip], 4)
+                emit(Q_OUT[ip], 4, False)
+            if ip in K_PARK:
+                back(K_PARK[ip], 4)
+                park(K_PARK[ip])
+            if ip == NPAIR + 1:
+                sumsq(4)
+                norm_a(1)
+                norm_b(1)
+        for h0, n in ((24, 4), (28, 2)):
+            back(h0, n)
+        emit(24, 4, False)
+        emit_parked(16)
+        emit(28, 2, True)
+        emit_parked(20)
+        back(30, 2)
+        emit(30, 2, True)

@@ -21,7 +21,6 @@ NPAIR = NH // 2
 PASSES = 4
 TT = 4
 EPS = 1e-6
-V_CAST = 1024
 FLOPS = 2 * S * 2 * DIM * DIM
 
 
@@ -166,11 +165,7 @@ def tile_dynamicselfattention_pa_kernel(
                     (DIM, 2 * DIM, nc.gpsimd.tensor_copy),
                 )
             else:
-                shares = (
-                    (0, V_CAST, nc.vector.tensor_copy),
-                    (V_CAST, DIM, nc.scalar.copy),
-                    (DIM, 2 * DIM, nc.scalar.copy),
-                )
+                shares = ((0, DIM, nc.scalar.copy), (DIM, 2 * DIM, nc.scalar.copy))
             for lo, hi, copy in shares:
                 copy(out=wide[:, lo:hi], in_=wb[:, lo:hi].bitcast(FP8))
             st[("wide", ip)] = wide
@@ -277,10 +272,11 @@ def tile_dynamicselfattention_pa_kernel(
             nc.vector.reciprocal(out=rstd[qk][:], in_=st[("rms", qk)][:])
 
         def products(ip, eng):
-            y = y_all[:, 2 * ip : 2 * ip + 2, :]
             z = zp.tile([P, 2, S], F32, name="z")
-            eng.tensor_tensor(out=z[:], in0=y, in1=sinT[:].to_broadcast([P, 2, S]), op=ALU.mult)
-            eng.tensor_tensor(out=y, in0=y, in1=cosT[:].to_broadcast([P, 2, S]), op=ALU.mult)
+            for a in range(2):
+                y = y_all[:, 2 * ip + a, :]
+                eng.tensor_tensor(out=z[:, a, :], in0=y, in1=sinT[:, 0, :], op=ALU.mult)
+                eng.tensor_tensor(out=y, in0=y, in1=cosT[:, 0, :], op=ALU.mult)
             st[("z", ip)] = z
 
         def back(h0, n):

@@ -21,6 +21,7 @@ NPAIR = NH // 2
 PASSES = 4
 TT = 4
 EPS = 1e-6
+V_CAST = 1024
 FLOPS = 2 * S * 2 * DIM * DIM
 
 
@@ -35,7 +36,8 @@ def tile_dynamicselfattention_pa_kernel(
         wbp = ctx.enter_context(tc.tile_pool(name="wbp", bufs=3))
         widep = ctx.enter_context(tc.tile_pool(name="widep", bufs=3))
         work = ctx.enter_context(tc.tile_pool(name="work", bufs=2))
-        sqp = ctx.enter_context(tc.tile_pool(name="sqp", bufs=10))
+        codep = ctx.enter_context(tc.tile_pool(name="codep", bufs=3))
+        sqp = ctx.enter_context(tc.tile_pool(name="sqp", bufs=14))
         zp = ctx.enter_context(tc.tile_pool(name="zp", bufs=10))
         obp = ctx.enter_context(tc.tile_pool(name="obp", bufs=8))
         psum = ctx.enter_context(tc.psum_pool(name="psum", bufs=7))
@@ -70,13 +72,17 @@ def tile_dynamicselfattention_pa_kernel(
 
         vecs = const.tile([P, P], BF16, name="vecs")
         nc.gpsimd.memset(vecs[:], 0.0)
-        nc.scalar.dma_start(out=vecs[0:32, :], in_=b_qk.rearrange("(h d) -> h d", d=HD))
-        nc.scalar.dma_start(out=vecs[32:48, :], in_=g_q.rearrange("(h d) -> h d", d=HD))
-        nc.scalar.dma_start(out=vecs[48:64, :], in_=g_k.rearrange("(h d) -> h d", d=HD))
+        nc.sync.dma_start(out=vecs[0:32, :], in_=b_qk.rearrange("(h d) -> h d", d=HD))
+        nc.sync.dma_start(out=vecs[32:48, :], in_=g_q.rearrange("(h d) -> h d", d=HD))
+        nc.sync.dma_start(out=vecs[48:64, :], in_=g_k.rearrange("(h d) -> h d", d=HD))
         cos_t = const.tile([P, TT, HD], BF16, name="cos_t")
         sin_t = const.tile([P, TT, HD], BF16, name="sin_t")
-        nc.scalar.dma_start(out=cos_t[:], in_=cos.rearrange("(j p) d -> p j d", p=P))
-        nc.scalar.dma_start(out=sin_t[:], in_=sin.rearrange("(j p) d -> p j d", p=P))
+        nc.sync.dma_start(out=cos_t[:], in_=cos.rearrange("(j p) d -> p j d", p=P))
+        nc.sync.dma_start(out=sin_t[:], in_=sin.rearrange("(j p) d -> p j d", p=P))
+
+        warm = const.tile([P, 1], F32, name="warm")
+        nc.vector.memset(warm[:], 0.0)
+        nc.scalar.activation(out=warm[:], in_=warm[:], func=ACT.Square)
 
         ident = const.tile([P, P], F32, name="ident")
         make_identity(nc, ident[:])
@@ -165,92 +171,95 @@ def tile_dynamicselfattention_pa_kernel(
                     (DIM, 2 * DIM, nc.gpsimd.tensor_copy),
                 )
             else:
-                shares = ((0, DIM, nc.scalar.copy), (DIM, 2 * DIM, nc.scalar.copy))
+                shares = (
+                    (0, V_CAST, nc.vector.tensor_copy),
+                    (V_CAST, DIM, nc.scalar.copy),
+                    (DIM, 2 * DIM, nc.scalar.copy),
+                )
             for lo, hi, copy in shares:
                 copy(out=wide[:, lo:hi], in_=wb[:, lo:hi].bitcast(FP8))
             st[("wide", ip)] = wide
 
-        def turn(ip):
-            words = st[("wide", ip)][:].bitcast(F32)
-            grouped = work.tile([P, 2 * DIM], BF16, name="grouped", align_bytes=64)
-            gv = grouped[:].rearrange("p (g m u e) -> p g m u e", g=PASSES, u=2, e=2)
-            for g in range(PASSES):
-                xt = psum.tile([P, 2, 2, P], F32, name="xt", tag="bank")
-                for a in range(2):
-                    for u in range(2):
-                        w0 = a * (DIM // 2) + 256 * g
-                        nc.tensor.transpose(
-                            xt[:, u, a, :], words[:, w0 + u : w0 + 256 : 2], ident[:]
-                        )
-                nc.vector.tensor_tensor(
-                    out=gv[:, g, :, :, :],
-                    in0=xt[:]
-                    .rearrange("p u a n -> p u (a n)")
-                    .bitcast(BF16)
-                    .rearrange("p u (m e) -> p m u e", e=2),
-                    in1=scale_t[:, g, :, :]
-                    .to_broadcast([P, 2 * P, 4])
-                    .rearrange("p m (u e) -> p m u e", e=2),
-                    op=ALU.mult,
+        def turn(ip, g):
+            if g == 0:
+                st[("grouped", ip)] = work.tile(
+                    [P, 2 * DIM], BF16, name="grouped", align_bytes=64
                 )
-            st[("grouped", ip)] = grouped
+            words = st[("wide", ip)][:].bitcast(F32)
+            gv = st[("grouped", ip)][:].rearrange(
+                "p (g m u e) -> p g m u e", g=PASSES, u=2, e=2
+            )
+            xt = psum.tile([P, 2, 2, P], F32, name="xt", tag="bank")
+            for a in range(2):
+                for u in range(2):
+                    w0 = a * (DIM // 2) + 256 * g
+                    nc.tensor.transpose(xt[:, u, a, :], words[:, w0 + u : w0 + 256 : 2], ident[:])
+            nc.vector.tensor_tensor(
+                out=gv[:, g, :, :, :],
+                in0=xt[:]
+                .rearrange("p u a n -> p u (a n)")
+                .bitcast(BF16)
+                .rearrange("p u (m e) -> p m u e", e=2),
+                in1=scale_t[:, g, :, :]
+                .to_broadcast([P, 2 * P, 4])
+                .rearrange("p m (u e) -> p m u e", e=2),
+                op=ALU.mult,
+            )
 
         def quantize(ip):
-            codes = work.tile([P, 2 * PASSES * P], U32, name="codes", align_bytes=64)
-            wsc = work.tile([P, 2 * PASSES * P], U8, name="wsc", align_bytes=64)
+            codes = codep.tile([P, 2 * PASSES * P], U32, name="codes", align_bytes=64)
+            wsc = codep.tile([P, 2 * PASSES * P], U8, name="wsc", align_bytes=64)
             nc.vector.quantize_mx(
                 out=codes[:].bitcast(FP8X4), scales=wsc[:], in_=st[("grouped", ip)][:]
             )
             st[("codes", ip)] = (codes, wsc)
 
-        def project(ip):
+        def project(ip, a):
             codes, wsc = st[("codes", ip)]
-            accs = []
-            for a in range(2):
-                acc = psum.tile([P, S], F32, name="acc", tag="bank")
-                accs.append(acc)
-                for g in range(PASSES):
-                    cols = slice((2 * g + a) * P, (2 * g + a + 1) * P)
-                    nc.tensor.matmul_mx(
-                        out=acc[:],
-                        lhsT=codes[:, cols].bitcast(FP8X4),
-                        lhsT_scale=wsc[:, cols],
-                        rhs=hs_codes[:, g * S : (g + 1) * S].bitcast(FP8X4),
-                        rhs_scale=hs_sc[:, g * S : (g + 1) * S],
-                        start=(g == 0),
-                        stop=(g == PASSES - 1),
-                    )
-            for a in range(2):
-                h = 2 * ip + a
-                nc.scalar.activation(
-                    out=y_all[:, h, :],
-                    in_=accs[a][:],
-                    func=ACT.Identity,
-                    bias=bgcol[:, h : h + 1],
-                    scale=gcol[:, h : h + 1],
+            h = 2 * ip + a
+            acc = psum.tile([P, S], F32, name="acc", tag="bank")
+            for g in range(PASSES):
+                cols = slice((2 * g + a) * P, (2 * g + a + 1) * P)
+                nc.tensor.matmul_mx(
+                    out=acc[:],
+                    lhsT=codes[:, cols].bitcast(FP8X4),
+                    lhsT_scale=wsc[:, cols],
+                    rhs=hs_codes[:, g * S : (g + 1) * S].bitcast(FP8X4),
+                    rhs_scale=hs_sc[:, g * S : (g + 1) * S],
+                    start=(g == 0),
+                    stop=(g == PASSES - 1),
                 )
-                sq = sqp.tile([P, S], F32, name="sq")
-                nc.scalar.activation(
-                    out=sq[:], in_=accs[a][:], func=ACT.Square, bias=bcol[:, h : h + 1], scale=1.0
-                )
-                st[("sq", h)] = sq
+            sq = sqp.tile([P, S], F32, name="sq")
+            nc.scalar.activation(
+                out=sq[:], in_=acc[:], func=ACT.Square, bias=bcol[:, h : h + 1], scale=1.0
+            )
+            st[("sq", h)] = sq
+            nc.scalar.activation(
+                out=y_all[:, h, :],
+                in_=acc[:],
+                func=ACT.Identity,
+                bias=bgcol[:, h : h + 1],
+                scale=gcol[:, h : h + 1],
+            )
 
         ROUNDS = ((0, 8), (8, 16), (16, 24), (24, 30), (30, 32))
 
-        def sumsq(r):
+        def sumsq(r, j):
             lo, hi = ROUNDS[r]
-            ssb = psum1.tile([P, TT, HD], F32, name="ssb")
-            for j in range(TT):
-                for h in range(lo, hi):
-                    nc.tensor.matmul(
-                        out=ssb[:, j, :],
-                        lhsT=st[("sq", h)][:, j * P : (j + 1) * P],
-                        rhs=ident[:],
-                        start=(h == lo),
-                        stop=(h == hi - 1),
-                        is_transpose=True,
-                    )
-            nc.vector.reduce_sum(out=part[:, r, :], in_=ssb[:], axis=mybir.AxisListType.X)
+            if j == 0:
+                st[("ssb", r)] = psum1.tile([P, TT, HD], F32, name="ssb")
+            ssb = st[("ssb", r)]
+            for h in range(lo, hi):
+                nc.tensor.matmul(
+                    out=ssb[:, j, :],
+                    lhsT=st[("sq", h)][:, j * P : (j + 1) * P],
+                    rhs=ident[:],
+                    start=(h == lo),
+                    stop=(h == hi - 1),
+                    is_transpose=True,
+                )
+            if j == TT - 1:
+                nc.vector.reduce_sum(out=part[:, r, :], in_=ssb[:], axis=mybir.AxisListType.X)
 
         def norm_a(qk):
             rounds = slice(0, 2) if qk == 0 else slice(2, 5)
@@ -279,115 +288,139 @@ def tile_dynamicselfattention_pa_kernel(
                 eng.tensor_tensor(out=y, in0=y, in1=cosT[:, 0, :], op=ALU.mult)
             st[("z", ip)] = z
 
-        def back(h0, n):
-            for j in range(TT):
-                ob = psum.tile([P, 4, HD], F32, name="ob", tag="bank")
-                st[("ob", h0, j)] = ob
-                for hh in range(n):
-                    h = h0 + hh
-                    nc.tensor.matmul(
-                        out=ob[:, hh, :],
-                        lhsT=y_all[:, h, j * P : (j + 1) * P],
-                        rhs=ident[:],
-                        start=True,
-                        stop=False,
-                        is_transpose=True,
-                    )
-                    nc.tensor.matmul(
-                        out=ob[:, hh, :],
-                        lhsT=st[("z", h // 2)][:, h % 2, j * P : (j + 1) * P],
-                        rhs=perm[:],
-                        start=False,
-                        stop=True,
-                        is_transpose=True,
-                    )
+        def back(h0, n, j):
+            ob = psum.tile([P, 4, HD], F32, name="ob", tag="bank")
+            for hh in range(n):
+                h = h0 + hh
+                nc.tensor.matmul(
+                    out=ob[:, hh, :],
+                    lhsT=y_all[:, h, j * P : (j + 1) * P],
+                    rhs=ident[:],
+                    start=True,
+                    stop=False,
+                    is_transpose=True,
+                )
+                nc.tensor.matmul(
+                    out=ob[:, hh, :],
+                    lhsT=st[("z", h // 2)][:, h % 2, j * P : (j + 1) * P],
+                    rhs=perm[:],
+                    start=False,
+                    stop=True,
+                    is_transpose=True,
+                )
+            return ob
 
-        def emit(h0, n, shared):
+        def store(h0, n, j, src):
             qk = h0 // 16
             c0 = (h0 % 16) * HD
             dst = outs[qk].rearrange("o (j p) h d -> p (o j) (h d)", p=P)
-            for j in range(TT):
-                obuf = obp.tile([P, 4, HD], F32, name="obuf")
-                ob = st[("ob", h0, j)]
-                if shared and j % 2 == 1:
-                    nc.vector.tensor_scalar(
-                        out=obuf[:, 0:n, :],
-                        in0=ob[:, 0:n, :],
-                        scalar1=rstd[qk][:, j : j + 1],
-                        scalar2=None,
-                        op0=ALU.mult,
-                    )
-                else:
-                    nc.scalar.activation(
-                        out=obuf[:, 0:n, :],
-                        in_=ob[:, 0:n, :],
-                        func=ACT.Copy,
-                        scale=rstd[qk][:, j : j + 1],
-                    )
-                nc.sync.dma_start(
-                    out=dst[:, j, c0 : c0 + n * HD],
-                    in_=obuf[:, 0:n, :].rearrange("p h d -> p (h d)"),
-                )
+            nc.sync.dma_start(out=dst[:, j, c0 : c0 + n * HD], in_=src)
 
-        def park(h0):
-            for j in range(TT):
-                nc.scalar.copy(
-                    out=y_all[:, h0 - 16 + j, :],
-                    in_=st[("ob", h0, j)][:].rearrange("p h d -> p (h d)"),
+        def emit(h0, n, j, on_vector):
+            ob = back(h0, n, j)
+            scale = rstd[h0 // 16][:, j : j + 1]
+            obuf = obp.tile([P, 4, HD], F32, name="obuf")
+            if on_vector:
+                nc.vector.tensor_scalar(
+                    out=obuf[:, 0:n, :],
+                    in0=ob[:, 0:n, :],
+                    scalar1=scale,
+                    scalar2=None,
+                    op0=ALU.mult,
                 )
+            else:
+                nc.scalar.activation(
+                    out=obuf[:, 0:n, :], in_=ob[:, 0:n, :], func=ACT.Copy, scale=scale
+                )
+            store(h0, n, j, obuf[:, 0:n, :].rearrange("p h d -> p (h d)"))
+
+        PLACE = {0: 24, 4: 28, 16: 0, 20: 4}
+
+        def park(h0, j):
+            ob = back(h0, 4, j)
+            nc.scalar.copy(
+                out=y_all[:, PLACE[h0] + j, :], in_=ob[:].rearrange("p h d -> p (h d)")
+            )
 
         def emit_parked(h0):
-            c0 = (h0 - 16) * HD
-            dst = outs[1].rearrange("o (j p) h d -> p (o j) (h d)", p=P)
             for j in range(TT):
-                y = y_all[:, h0 - 16 + j, :]
+                y = y_all[:, PLACE[h0] + j, :]
                 nc.vector.tensor_scalar(
-                    out=y, in0=y, scalar1=rstd[1][:, j : j + 1], scalar2=None, op0=ALU.mult
+                    out=y,
+                    in0=y,
+                    scalar1=rstd[h0 // 16][:, j : j + 1],
+                    scalar2=None,
+                    op0=ALU.mult,
                 )
-                nc.sync.dma_start(out=dst[:, j, c0 : c0 + 4 * HD], in_=y)
+                store(h0, 4, j, y)
 
-        Q_OUT = {12: 0, 13: 4, 14: 8, 15: 12}
-        K_PARK = {16: 16, 17: 20}
-        for ip in range(NPAIR + 3):
-            if ip < NPAIR:
-                cast(ip)
-                if ip + 3 < NPAIR:
-                    load_w(ip + 3)
-            if 0 <= ip - 2 < NPAIR:
-                quantize(ip - 2)
-            if 0 <= ip - 1 < NPAIR:
-                turn(ip - 1)
+        EXTRAS = {
+            7: [(sumsq, 0, 0), (sumsq, 0, 1), (park, 0, 0)],
+            8: [(sumsq, 0, 2), (sumsq, 0, 3), (park, 0, 1)],
+            9: [(park, 0, 2), (park, 0, 3), (park, 4, 0)],
+            10: [(park, 4, 1), (park, 4, 2), (park, 4, 3)],
+            11: [(sumsq, 1, 0), (sumsq, 1, 1)],
+            12: [(sumsq, 1, 2), (sumsq, 1, 3)],
+            13: [(emit, 8, 4, 0, False), (emit, 8, 4, 1, False), (emit, 8, 4, 2, False)],
+            14: [(emit, 8, 4, 3, False), (emit, 12, 4, 0, False), (emit, 12, 4, 1, False)],
+            15: [(emit, 12, 4, 2, False), (emit, 12, 4, 3, False), (sumsq, 2, 0)],
+            16: [(sumsq, 2, 1), (sumsq, 2, 2), (sumsq, 2, 3), (park, 16, 0)],
+        }
+        ctx.enter_context(tc.manual_schedule(engines={mybir.EngineType.PE}))
+        cast(0)
+        cast(1)
+        for ip in range(1, NPAIR + 1):
+            if ip + 1 < NPAIR:
+                cast(ip + 1)
+            if 2 < ip + 2 < NPAIR:
+                load_w(ip + 2)
+            extras = EXTRAS.get(ip, [])
+            for a in range(2):
+                turn(ip - 1, 2 * a)
+                turn(ip - 1, 2 * a + 1)
+                if a == 0 and ip >= 2:
+                    quantize(ip - 2)
+                if ip >= 3:
+                    project(ip - 3, a)
+                for x in extras[2 * a : 2 * a + 2]:
+                    x[0](*x[1:])
             if ip == 1:
                 turn_hidden()
                 quantize_hidden()
                 columns()
             if ip == 2:
                 rope_tables()
-            if ip in (6, 10, 14, 17):
-                sumsq({6: 0, 10: 1, 14: 2, 17: 3}[ip])
-            if 0 <= ip - 2 < NPAIR:
-                project(ip - 2)
-            if 0 <= ip - 3 < NPAIR:
-                products(ip - 3, nc.gpsimd if ip - 3 < NPAIR - 2 else nc.vector)
-            if ip == 10:
+            if ip >= 4:
+                products(ip - 4, nc.gpsimd)
+            if ip == 12:
                 norm_a(0)
-            if ip == 11:
                 norm_b(0)
-            if ip in Q_OUT:
-                back(Q_OUT[ip], 4)
-                emit(Q_OUT[ip], 4, False)
-            if ip in K_PARK:
-                back(K_PARK[ip], 4)
-                park(K_PARK[ip])
-            if ip == NPAIR + 1:
-                sumsq(4)
-                norm_a(1)
-                norm_b(1)
-        for h0, n in ((24, 4), (28, 2)):
-            back(h0, n)
-        emit(24, 4, False)
+                emit_parked(0)
+            if ip == 13:
+                emit_parked(4)
+        quantize(NPAIR - 1)
+        products(NPAIR - 3, nc.gpsimd)
+        for a in range(2):
+            project(NPAIR - 2, a)
+        for j in range(1, TT):
+            park(16, j)
+        for a in range(2):
+            project(NPAIR - 1, a)
+        for j in range(TT):
+            sumsq(3, j)
+        for j in range(TT):
+            park(20, j)
+        for j in range(TT):
+            sumsq(4, j)
+        norm_a(1)
+        norm_b(1)
+        products(NPAIR - 2, nc.vector)
+        products(NPAIR - 1, nc.vector)
+        for j in range(TT):
+            emit(24, 4, j, False)
         emit_parked(16)
-        emit(28, 2, True)
+        for j in range(TT):
+            emit(28, 2, j, j % 2 == 1)
         emit_parked(20)
-        back(30, 2)
-        emit(30, 2, True)
+        for j in range(TT):
+            emit(30, 2, j, j % 2 == 1)

@@ -21,7 +21,7 @@ NPAIR = NH // 2
 PASSES = 4
 TT = 4
 EPS = 1e-6
-V_CAST = 1024
+G_CAST = 1536
 FLOPS = 2 * S * 2 * DIM * DIM
 
 
@@ -59,6 +59,7 @@ def tile_dynamicselfattention_pa_kernel(
             out=scale_t[:].rearrange("p g o t -> p (g o) t"),
             in_=w_qk_scale.rearrange("o (g p t) -> p (o g) t", p=P, t=4),
         )
+        load_w(1)
         hs_view = hidden_states.rearrange("o (j p) k -> (o j) p k", p=P)
         hs_tiles = []
         for j in range(TT):
@@ -67,8 +68,6 @@ def tile_dynamicselfattention_pa_kernel(
             )
             nc.sync.dma_start(out=hs_t[:], in_=hs_view[j])
             hs_tiles.append(hs_t)
-        load_w(1)
-        load_w(2)
 
         vecs = const.tile([P, P], BF16, name="vecs")
         nc.gpsimd.memset(vecs[:], 0.0)
@@ -79,6 +78,7 @@ def tile_dynamicselfattention_pa_kernel(
         sin_t = const.tile([P, TT, HD], BF16, name="sin_t")
         nc.sync.dma_start(out=cos_t[:], in_=cos.rearrange("(j p) d -> p j d", p=P))
         nc.sync.dma_start(out=sin_t[:], in_=sin.rearrange("(j p) d -> p j d", p=P))
+        load_w(2)
 
         warm = const.tile([P, 1], F32, name="warm")
         nc.vector.memset(warm[:], 0.0)
@@ -97,8 +97,8 @@ def tile_dynamicselfattention_pa_kernel(
         hs_codes = const.tile([P, PASSES * S], U32, name="hs_codes", align_bytes=64)
         hs_sc = const.tile([P, PASSES * S], U8, name="hs_sc", align_bytes=64)
 
-        def turn_hidden():
-            for j in range(TT):
+        def turn_hidden(tiles):
+            for j in tiles:
                 words = hs_tiles[j][:].bitcast(F32)
                 for b in range(2):
                     xt = psum.tile([P, 512], F32, name="xt", tag="bank")
@@ -133,21 +133,20 @@ def tile_dynamicselfattention_pa_kernel(
             nc.tensor.transpose(vt[:], vecs[:], ident_bf[:])
             nc.scalar.copy(out=bcol[:], in_=vt[:, 0:32])
             nc.scalar.copy(out=gcol[:], in_=vt[:, 32:64])
-            nc.gpsimd.tensor_tensor(out=bgcol[:], in0=bcol[:], in1=gcol[:], op=ALU.mult)
+            nc.vector.tensor_tensor(out=bgcol[:], in0=bcol[:], in1=gcol[:], op=ALU.mult)
 
         cosT = const.tile([P, 1, S], BF16, name="cosT")
         sinT = const.tile([P, 1, S], BF16, name="sinT")
 
         def rope_tables():
             sinsw = const.tile([P, TT, HD], BF16, name="sinsw")
-            nc.gpsimd.tensor_copy(out=sinsw[:, :, 0:64], in_=sin_t[:, :, 64:128])
-            nc.gpsimd.tensor_scalar(
+            nc.vector.tensor_copy(out=sinsw[:, :, 0:64], in_=sin_t[:, :, 64:128])
+            nc.vector.tensor_scalar(
                 out=sinsw[:, :, 64:128],
                 in0=sin_t[:, :, 0:64],
                 scalar1=-1.0,
-                scalar2=0.0,
+                scalar2=None,
                 op0=ALU.mult,
-                op1=ALU.add,
             )
             for src_t, dst_t in ((cos_t, cosT), (sinsw, sinT)):
                 tb = psum.tile([P, S], BF16, name="tb", tag="bank")
@@ -162,9 +161,14 @@ def tile_dynamicselfattention_pa_kernel(
 
         def cast(ip):
             wide = widep.tile([P, 2 * DIM], BF16, name="wide")
+            st[("wide", ip)] = wide
             wb = wb_tiles[ip][:].rearrange("p a k -> p (a k)")
             if ip == 0:
-                shares = ((0, DIM, nc.vector.tensor_copy), (DIM, 2 * DIM, nc.scalar.copy))
+                shares = (
+                    (0, DIM, nc.vector.tensor_copy),
+                    (DIM, DIM + DIM // 2, nc.scalar.copy),
+                    (DIM + DIM // 2, 2 * DIM, nc.gpsimd.tensor_copy),
+                )
             elif ip <= 2:
                 shares = (
                     (0, DIM, nc.gpsimd.tensor_copy),
@@ -172,13 +176,12 @@ def tile_dynamicselfattention_pa_kernel(
                 )
             else:
                 shares = (
-                    (0, V_CAST, nc.vector.tensor_copy),
-                    (V_CAST, DIM, nc.scalar.copy),
-                    (DIM, 2 * DIM, nc.scalar.copy),
+                    (0, DIM, nc.scalar.copy),
+                    (DIM, 2 * DIM - G_CAST, nc.scalar.copy),
+                    (2 * DIM - G_CAST, 2 * DIM, nc.gpsimd.tensor_copy),
                 )
             for lo, hi, copy in shares:
                 copy(out=wide[:, lo:hi], in_=wb[:, lo:hi].bitcast(FP8))
-            st[("wide", ip)] = wide
 
         def turn(ip, g):
             if g == 0:
@@ -234,20 +237,32 @@ def tile_dynamicselfattention_pa_kernel(
                 out=sq[:], in_=acc[:], func=ACT.Square, bias=bcol[:, h : h + 1], scale=1.0
             )
             st[("sq", h)] = sq
-            nc.scalar.activation(
-                out=y_all[:, h, :],
-                in_=acc[:],
-                func=ACT.Identity,
-                bias=bgcol[:, h : h + 1],
-                scale=gcol[:, h : h + 1],
-            )
+            if ip == NPAIR - 1:
+                nc.vector.tensor_scalar(
+                    out=y_all[:, h, :],
+                    in0=acc[:],
+                    scalar1=gcol[:, h : h + 1],
+                    scalar2=bgcol[:, h : h + 1],
+                    op0=ALU.mult,
+                    op1=ALU.add,
+                )
+            else:
+                nc.scalar.activation(
+                    out=y_all[:, h, :],
+                    in_=acc[:],
+                    func=ACT.Identity,
+                    bias=bgcol[:, h : h + 1],
+                    scale=gcol[:, h : h + 1],
+                )
 
-        ROUNDS = ((0, 8), (8, 16), (16, 24), (24, 30), (30, 32))
+        ROUNDS = ((0, 8), (8, 16), (16, 24), (24, 28), (28, 32))
 
         def sumsq(r, j):
             lo, hi = ROUNDS[r]
-            if j == 0:
+            if j == 0 and r < 4:
                 st[("ssb", r)] = psum1.tile([P, TT, HD], F32, name="ssb")
+            elif j == 0:
+                st[("ssb", r)] = psum.tile([P, TT, HD], F32, name="ssb2", tag="bank")
             ssb = st[("ssb", r)]
             for h in range(lo, hi):
                 nc.tensor.matmul(
@@ -280,13 +295,19 @@ def tile_dynamicselfattention_pa_kernel(
         def norm_b(qk):
             nc.vector.reciprocal(out=rstd[qk][:], in_=st[("rms", qk)][:])
 
-        def products(ip, eng):
+        def sine(ip):
             z = zp.tile([P, 2, S], F32, name="z")
-            for a in range(2):
-                y = y_all[:, 2 * ip + a, :]
-                eng.tensor_tensor(out=z[:, a, :], in0=y, in1=sinT[:, 0, :], op=ALU.mult)
-                eng.tensor_tensor(out=y, in0=y, in1=cosT[:, 0, :], op=ALU.mult)
+            nc.vector.tensor_tensor(
+                out=z[:],
+                in0=y_all[:, 2 * ip : 2 * ip + 2, :],
+                in1=sinT[:].to_broadcast([P, 2, S]),
+                op=ALU.mult,
+            )
             st[("z", ip)] = z
+
+        def cosine(ip, eng):
+            y = y_all[:, 2 * ip : 2 * ip + 2, :]
+            eng.tensor_tensor(out=y, in0=y, in1=cosT[:].to_broadcast([P, 2, S]), op=ALU.mult)
 
         def back(h0, n, j):
             ob = psum.tile([P, 4, HD], F32, name="ob", tag="bank")
@@ -334,7 +355,7 @@ def tile_dynamicselfattention_pa_kernel(
                 )
             store(h0, n, j, obuf[:, 0:n, :].rearrange("p h d -> p (h d)"))
 
-        PLACE = {0: 24, 4: 28, 16: 0, 20: 4}
+        PLACE = {0: 24, 4: 28}
 
         def park(h0, j):
             ob = back(h0, 4, j)
@@ -355,72 +376,83 @@ def tile_dynamicselfattention_pa_kernel(
                 store(h0, 4, j, y)
 
         EXTRAS = {
-            7: [(sumsq, 0, 0), (sumsq, 0, 1), (park, 0, 0)],
-            8: [(sumsq, 0, 2), (sumsq, 0, 3), (park, 0, 1)],
-            9: [(park, 0, 2), (park, 0, 3), (park, 4, 0)],
-            10: [(park, 4, 1), (park, 4, 2), (park, 4, 3)],
-            11: [(sumsq, 1, 0), (sumsq, 1, 1)],
-            12: [(sumsq, 1, 2), (sumsq, 1, 3)],
-            13: [(emit, 8, 4, 0, False), (emit, 8, 4, 1, False), (emit, 8, 4, 2, False)],
-            14: [(emit, 8, 4, 3, False), (emit, 12, 4, 0, False), (emit, 12, 4, 1, False)],
-            15: [(emit, 12, 4, 2, False), (emit, 12, 4, 3, False), (sumsq, 2, 0)],
-            16: [(sumsq, 2, 1), (sumsq, 2, 2), (sumsq, 2, 3), (park, 16, 0)],
+            6: [(park, 0, 0), (park, 0, 1)],
+            7: [(sumsq, 0, 0), (sumsq, 0, 1), (park, 0, 2)],
+            8: [(sumsq, 0, 2), (sumsq, 0, 3), (park, 0, 3)],
+            9: [(park, 4, 0), (park, 4, 1)],
+            10: [(park, 4, 2), (park, 4, 3), (sumsq, 1, 0)],
+            11: [(sumsq, 1, 1), (sumsq, 1, 2), (sumsq, 1, 3)],
+            12: [(emit, 8, 4, 0, False), (emit, 8, 4, 1, False)],
+            13: [(emit, 8, 4, 2, False), (emit, 8, 4, 3, False)],
+            14: [(emit, 12, 4, 0, False), (emit, 12, 4, 1, False), (sumsq, 2, 0)],
+            15: [(emit, 12, 4, 2, False), (emit, 12, 4, 3, False), (sumsq, 2, 1)],
         }
-        ctx.enter_context(tc.manual_schedule(engines={mybir.EngineType.PE}))
+        ctx.enter_context(
+            tc.manual_schedule(
+                engines={
+                    mybir.EngineType.PE,
+                    mybir.EngineType.DVE,
+                    mybir.EngineType.Pool,
+                    mybir.EngineType.Activation,
+                }
+            )
+        )
         cast(0)
         cast(1)
-        for ip in range(1, NPAIR + 1):
-            if ip + 1 < NPAIR:
-                cast(ip + 1)
-            if 2 < ip + 2 < NPAIR:
-                load_w(ip + 2)
-            extras = EXTRAS.get(ip, [])
-            for a in range(2):
-                turn(ip - 1, 2 * a)
-                turn(ip - 1, 2 * a + 1)
-                if a == 0 and ip >= 2:
-                    quantize(ip - 2)
-                if ip >= 3:
-                    project(ip - 3, a)
-                for x in extras[2 * a : 2 * a + 2]:
-                    x[0](*x[1:])
-            if ip == 1:
-                turn_hidden()
-                quantize_hidden()
-                columns()
-            if ip == 2:
-                rope_tables()
+        cast(2)
+        load_w(3)
+        for g in range(PASSES):
+            turn(0, g)
+        turn_hidden((0, 1, 2))
+        for g in range(PASSES):
+            turn(1, g)
+        turn_hidden((3,))
+        columns()
+        rope_tables()
+        quantize_hidden()
+        quantize(0)
+        for ip in range(3, NPAIR + 1):
+            quantize(ip - 2)
             if ip >= 4:
-                products(ip - 4, nc.gpsimd)
-            if ip == 12:
+                sine(ip - 4)
+                cosine(ip - 4, nc.gpsimd)
+            for c in (3, 4) if ip == 3 else (ip + 1,):
+                if c < NPAIR:
+                    cast(c)
+                    if c + 1 < NPAIR:
+                        load_w(c + 1)
+            for g in range(PASSES):
+                turn(ip - 1, g)
+                if ip == 12 and g == 1:
+                    norm_b(0)
+            for x in EXTRAS.get(ip, []):
+                x[0](*x[1:])
+            for c in (0, 1) if ip == 3 else (ip - 2,):
+                for a in range(2):
+                    project(c, a)
+            if ip == 11:
                 norm_a(0)
-                norm_b(0)
+            if ip == 12:
                 emit_parked(0)
             if ip == 13:
                 emit_parked(4)
         quantize(NPAIR - 1)
-        products(NPAIR - 3, nc.gpsimd)
-        for a in range(2):
-            project(NPAIR - 2, a)
-        for j in range(1, TT):
-            park(16, j)
+        for j in (2, 3):
+            sumsq(2, j)
+        sine(NPAIR - 3)
+        cosine(NPAIR - 3, nc.gpsimd)
         for a in range(2):
             project(NPAIR - 1, a)
         for j in range(TT):
             sumsq(3, j)
-        for j in range(TT):
-            park(20, j)
+        sine(NPAIR - 2)
+        cosine(NPAIR - 2, nc.vector)
         for j in range(TT):
             sumsq(4, j)
         norm_a(1)
         norm_b(1)
-        products(NPAIR - 2, nc.vector)
-        products(NPAIR - 1, nc.vector)
-        for j in range(TT):
-            emit(24, 4, j, False)
-        emit_parked(16)
-        for j in range(TT):
-            emit(28, 2, j, j % 2 == 1)
-        emit_parked(20)
-        for j in range(TT):
-            emit(30, 2, j, j % 2 == 1)
+        sine(NPAIR - 1)
+        cosine(NPAIR - 1, nc.vector)
+        for h0 in (16, 20, 24, 28):
+            for j in range(TT):
+                emit(h0, 4, j, j % 2 == 1)

@@ -36,10 +36,11 @@ def tile_dynamicselfattention_pa_kernel(
         wbp = ctx.enter_context(tc.tile_pool(name="wbp", bufs=3))
         widep = ctx.enter_context(tc.tile_pool(name="widep", bufs=3))
         work = ctx.enter_context(tc.tile_pool(name="work", bufs=2))
-        codep = ctx.enter_context(tc.tile_pool(name="codep", bufs=3))
+        codep = ctx.enter_context(tc.tile_pool(name="codep", bufs=2))
         sqp = ctx.enter_context(tc.tile_pool(name="sqp", bufs=14))
-        zp = ctx.enter_context(tc.tile_pool(name="zp", bufs=10))
-        obp = ctx.enter_context(tc.tile_pool(name="obp", bufs=8))
+        zp = ctx.enter_context(tc.tile_pool(name="zp", bufs=7))
+        tokp = ctx.enter_context(tc.tile_pool(name="tokp", bufs=3))
+        obp = ctx.enter_context(tc.tile_pool(name="obp", bufs=10))
         psum = ctx.enter_context(tc.psum_pool(name="psum", bufs=7))
         psum1 = ctx.enter_context(tc.psum_pool(name="psum1", bufs=1))
 
@@ -80,6 +81,8 @@ def tile_dynamicselfattention_pa_kernel(
         nc.sync.dma_start(out=sin_t[:], in_=sin.rearrange("(j p) d -> p j d", p=P))
         load_w(2)
 
+        eps_t = const.tile([P, 1], F32, name="eps_t")
+        nc.gpsimd.memset(eps_t[:], EPS)
         warm = const.tile([P, 1], F32, name="warm")
         nc.vector.memset(warm[:], 0.0)
         nc.scalar.activation(out=warm[:], in_=warm[:], func=ACT.Square)
@@ -133,13 +136,17 @@ def tile_dynamicselfattention_pa_kernel(
             nc.tensor.transpose(vt[:], vecs[:], ident_bf[:])
             nc.scalar.copy(out=bcol[:], in_=vt[:, 0:32])
             nc.scalar.copy(out=gcol[:], in_=vt[:, 32:64])
-            nc.vector.tensor_tensor(out=bgcol[:], in0=bcol[:], in1=gcol[:], op=ALU.mult)
 
         cosT = const.tile([P, 1, S], BF16, name="cosT")
         sinT = const.tile([P, 1, S], BF16, name="sinT")
 
-        def rope_tables():
-            sinsw = const.tile([P, TT, HD], BF16, name="sinsw")
+        sinsw = const.tile([P, TT, HD], BF16, name="sinsw")
+        sinsg = const.tile([P, TT, HD], BF16, name="sinsg")
+        cosn = const.tile([P, TT, HD], F32, name="cosn")
+        sinn = const.tile([P, TT, HD], F32, name="sinn")
+
+        def small_vector_work():
+            nc.vector.tensor_tensor(out=bgcol[:], in0=bcol[:], in1=gcol[:], op=ALU.mult)
             nc.vector.tensor_copy(out=sinsw[:, :, 0:64], in_=sin_t[:, :, 64:128])
             nc.vector.tensor_scalar(
                 out=sinsw[:, :, 64:128],
@@ -148,6 +155,18 @@ def tile_dynamicselfattention_pa_kernel(
                 scalar2=None,
                 op0=ALU.mult,
             )
+
+        def token_table():
+            nc.vector.tensor_scalar(
+                out=sinsg[:, :, 0:64],
+                in0=sin_t[:, :, 0:64],
+                scalar1=-1.0,
+                scalar2=None,
+                op0=ALU.mult,
+            )
+            nc.vector.tensor_copy(out=sinsg[:, :, 64:128], in_=sin_t[:, :, 64:128])
+
+        def rope_tables():
             for src_t, dst_t in ((cos_t, cosT), (sinsw, sinT)):
                 tb = psum.tile([P, S], BF16, name="tb", tag="bank")
                 for j in range(TT):
@@ -158,6 +177,9 @@ def tile_dynamicselfattention_pa_kernel(
         part = const.tile([P, 5, TT], F32, name="part")
         rstd = [const.tile([P, TT], F32, name="rstd%d" % i) for i in range(2)]
         st = {}
+
+        def sorted_head(ip):
+            return ip >= 5 and ip % 2 == 1
 
         def cast(ip):
             wide = widep.tile([P, 2 * DIM], BF16, name="wide")
@@ -170,10 +192,9 @@ def tile_dynamicselfattention_pa_kernel(
                     (DIM + DIM // 2, 2 * DIM, nc.gpsimd.tensor_copy),
                 )
             elif ip <= 2:
-                shares = (
-                    (0, DIM, nc.gpsimd.tensor_copy),
-                    (DIM, 2 * DIM, nc.gpsimd.tensor_copy),
-                )
+                shares = ((0, DIM, nc.gpsimd.tensor_copy), (DIM, 2 * DIM, nc.scalar.copy))
+            elif ip <= 4:
+                shares = ((0, DIM, nc.scalar.copy), (DIM, 2 * DIM, nc.scalar.copy))
             else:
                 shares = (
                     (0, DIM, nc.scalar.copy),
@@ -182,6 +203,15 @@ def tile_dynamicselfattention_pa_kernel(
                 )
             for lo, hi, copy in shares:
                 copy(out=wide[:, lo:hi], in_=wb[:, lo:hi].bitcast(FP8))
+            if sorted_head(ip):
+                sw = work.tile([P, DIM // 2], F32, name="sw")
+                nc.scalar.copy(
+                    out=sw[:].rearrange("p (g u q) -> p g u q", g=PASSES, u=2),
+                    in_=wide[:, 0:DIM]
+                    .bitcast(F32)
+                    .rearrange("p (g q u) -> p g u q", g=PASSES, u=2),
+                )
+                st[("sw", ip)] = sw
 
         def turn(ip, g):
             if g == 0:
@@ -196,7 +226,10 @@ def tile_dynamicselfattention_pa_kernel(
             for a in range(2):
                 for u in range(2):
                     w0 = a * (DIM // 2) + 256 * g
-                    nc.tensor.transpose(xt[:, u, a, :], words[:, w0 + u : w0 + 256 : 2], ident[:])
+                    src = words[:, w0 + u : w0 + 256 : 2]
+                    if a == 0 and sorted_head(ip):
+                        src = st[("sw", ip)][:, w0 + u * P : w0 + (u + 1) * P]
+                    nc.tensor.transpose(xt[:, u, a, :], src, ident[:])
             nc.vector.tensor_tensor(
                 out=gv[:, g, :, :, :],
                 in0=xt[:]
@@ -255,7 +288,7 @@ def tile_dynamicselfattention_pa_kernel(
                     scale=gcol[:, h : h + 1],
                 )
 
-        ROUNDS = ((0, 8), (8, 16), (16, 24), (24, 28), (28, 32))
+        ROUNDS = ((0, 8), (8, 16), (16, 24), (24, 30), (30, 32))
 
         def sumsq(r, j):
             lo, hi = ROUNDS[r]
@@ -273,8 +306,17 @@ def tile_dynamicselfattention_pa_kernel(
                     stop=(h == hi - 1),
                     is_transpose=True,
                 )
-            if j == TT - 1:
-                nc.vector.reduce_sum(out=part[:, r, :], in_=ssb[:], axis=mybir.AxisListType.X)
+            if r >= 3:
+                if j == TT - 1:
+                    nc.vector.reduce_sum(out=part[:, r, :], in_=ssb[:], axis=mybir.AxisListType.X)
+            else:
+                junk = work.tile([P, HD], F32, name="junk")
+                nc.scalar.activation(
+                    out=junk[:],
+                    in_=ssb[:, j, :],
+                    func=ACT.Copy,
+                    accum_out=part[:, r, j : j + 1],
+                )
 
         def norm_a(qk):
             rounds = slice(0, 2) if qk == 0 else slice(2, 5)
@@ -284,12 +326,10 @@ def tile_dynamicselfattention_pa_kernel(
                 in_=part[:, rounds, :].rearrange("p r j -> p j r"),
                 axis=mybir.AxisListType.X,
             )
-            ms = work.tile([P, TT], F32, name="ms")
-            nc.vector.tensor_scalar(
-                out=ms[:], in0=ssum[:], scalar1=1.0 / DIM, scalar2=EPS, op0=ALU.mult, op1=ALU.add
-            )
             rms = work.tile([P, TT], F32, name="rms")
-            nc.scalar.activation(out=rms[:], in_=ms[:], func=ACT.Sqrt)
+            nc.scalar.activation(
+                out=rms[:], in_=ssum[:], func=ACT.Sqrt, bias=eps_t[:], scale=1.0 / DIM
+            )
             st[("rms", qk)] = rms
 
         def norm_b(qk):
@@ -338,7 +378,12 @@ def tile_dynamicselfattention_pa_kernel(
             nc.sync.dma_start(out=dst[:, j, c0 : c0 + n * HD], in_=src)
 
         def emit(h0, n, j, on_vector):
-            ob = back(h0, n, j)
+            flush(h0, n, j, on_vector, back(h0, n, j))
+
+        def flush_scalar(h0, j, ob):
+            flush(h0, 4, j, False, ob)
+
+        def flush(h0, n, j, on_vector, ob):
             scale = rstd[h0 // 16][:, j : j + 1]
             obuf = obp.tile([P, 4, HD], F32, name="obuf")
             if on_vector:
@@ -355,7 +400,44 @@ def tile_dynamicselfattention_pa_kernel(
                 )
             store(h0, n, j, obuf[:, 0:n, :].rearrange("p h d -> p (h d)"))
 
-        PLACE = {0: 24, 4: 28}
+        def turn_y(h0, j):
+            ob = psum.tile([P, 4, HD], F32, name="ob", tag="bank")
+            for hh in range(4):
+                nc.tensor.transpose(ob[:, hh, :], y_all[:, h0 + hh, j * P : (j + 1) * P], ident[:])
+            return ob
+
+        def rope_tokens(h0, j, ob):
+            if h0 == 24:
+                for src_t, dst_t in ((cos_t, cosn), (sinsg, sinn)):
+                    nc.vector.tensor_scalar(
+                        out=dst_t[:, j, :],
+                        in0=src_t[:, j, :],
+                        scalar1=rstd[1][:, j : j + 1],
+                        scalar2=None,
+                        op0=ALU.mult,
+                    )
+            ta = obp.tile([P, 4, HD], F32, name="obuf")
+            tz = tokp.tile([P, 4, HD], F32, name="tz")
+            nc.vector.tensor_tensor(
+                out=ta[:],
+                in0=ob[:],
+                in1=cosn[:, j : j + 1, :].to_broadcast([P, 4, HD]),
+                op=ALU.mult,
+            )
+            halves = ob[:].rearrange("p h (b d) -> p h b d", b=2)
+            nc.vector.tensor_tensor(
+                out=tz[:].rearrange("p h (b d) -> p h b d", b=2),
+                in0=halves[:, :, ::-1, :],
+                in1=sinn[:, j : j + 1, :]
+                .to_broadcast([P, 4, HD])
+                .rearrange("p h (b d) -> p h b d", b=2),
+                op=ALU.mult,
+            )
+            adder = nc.vector if h0 == 28 and j >= 2 else nc.gpsimd
+            adder.tensor_tensor(out=ta[:], in0=ta[:], in1=tz[:], op=ALU.add)
+            store(h0, 4, j, ta[:].rearrange("p h d -> p (h d)"))
+
+        PLACE = {0: 28, 4: 0}
 
         def park(h0, j):
             ob = back(h0, 4, j)
@@ -363,29 +445,29 @@ def tile_dynamicselfattention_pa_kernel(
                 out=y_all[:, PLACE[h0] + j, :], in_=ob[:].rearrange("p h d -> p (h d)")
             )
 
-        def emit_parked(h0):
-            for j in range(TT):
-                y = y_all[:, PLACE[h0] + j, :]
+        def emit_parked(h0, j, on_vector):
+            y = y_all[:, PLACE[h0] + j, :]
+            scale = rstd[h0 // 16][:, j : j + 1]
+            if on_vector:
                 nc.vector.tensor_scalar(
-                    out=y,
-                    in0=y,
-                    scalar1=rstd[h0 // 16][:, j : j + 1],
-                    scalar2=None,
-                    op0=ALU.mult,
+                    out=y, in0=y, scalar1=scale, scalar2=None, op0=ALU.mult
                 )
-                store(h0, 4, j, y)
+            else:
+                nc.scalar.activation(out=y, in_=y, func=ACT.Copy, scale=scale)
+            store(h0, 4, j, y)
 
         EXTRAS = {
             6: [(park, 0, 0), (park, 0, 1)],
             7: [(sumsq, 0, 0), (sumsq, 0, 1), (park, 0, 2)],
-            8: [(sumsq, 0, 2), (sumsq, 0, 3), (park, 0, 3)],
-            9: [(park, 4, 0), (park, 4, 1)],
-            10: [(park, 4, 2), (park, 4, 3), (sumsq, 1, 0)],
-            11: [(sumsq, 1, 1), (sumsq, 1, 2), (sumsq, 1, 3)],
-            12: [(emit, 8, 4, 0, False), (emit, 8, 4, 1, False)],
-            13: [(emit, 8, 4, 2, False), (emit, 8, 4, 3, False)],
-            14: [(emit, 12, 4, 0, False), (emit, 12, 4, 1, False), (sumsq, 2, 0)],
-            15: [(emit, 12, 4, 2, False), (emit, 12, 4, 3, False), (sumsq, 2, 1)],
+            8: [(sumsq, 0, 2), (sumsq, 0, 3)],
+            9: [(park, 0, 3), (park, 4, 0)],
+            10: [(sumsq, 1, 0), (sumsq, 1, 1), (sumsq, 1, 2)],
+            11: [(sumsq, 1, 3), (park, 4, 1)],
+            12: [(park, 4, 2), (park, 4, 3)],
+            13: [(emit, 8, 4, 0, False), (emit, 8, 4, 1, False)],
+            14: [(emit, 8, 4, 2, False), (emit, 8, 4, 3, False)],
+            15: [(emit, 12, 4, 0, False), (emit, 12, 4, 1, False), (sumsq, 2, 0)],
+            16: [(sumsq, 2, 1)],
         }
         ctx.enter_context(
             tc.manual_schedule(
@@ -399,60 +481,73 @@ def tile_dynamicselfattention_pa_kernel(
         )
         cast(0)
         cast(1)
-        cast(2)
-        load_w(3)
         for g in range(PASSES):
             turn(0, g)
-        turn_hidden((0, 1, 2))
+        turn_hidden((0, 1))
         for g in range(PASSES):
             turn(1, g)
-        turn_hidden((3,))
-        columns()
-        rope_tables()
+        turn_hidden((2, 3))
+        cast(2)
+        load_w(3)
         quantize_hidden()
         quantize(0)
+        columns()
         for ip in range(3, NPAIR + 1):
             quantize(ip - 2)
-            if ip >= 4:
+            if ip == 3:
+                small_vector_work()
+            if ip == 13:
+                norm_b(0)
+            if ip == 9:
+                token_table()
+            if 4 <= ip < 16:
                 sine(ip - 4)
                 cosine(ip - 4, nc.gpsimd)
-            for c in (3, 4) if ip == 3 else (ip + 1,):
-                if c < NPAIR:
-                    cast(c)
-                    if c + 1 < NPAIR:
-                        load_w(c + 1)
+            c = 3 if ip == 3 else ip + 1
+            if c < NPAIR:
+                cast(c)
+                if c + 1 < NPAIR:
+                    load_w(c + 1)
             for g in range(PASSES):
                 turn(ip - 1, g)
-                if ip == 12 and g == 1:
-                    norm_b(0)
             for x in EXTRAS.get(ip, []):
                 x[0](*x[1:])
-            for c in (0, 1) if ip == 3 else (ip - 2,):
+            if ip == 3:
                 for a in range(2):
-                    project(c, a)
+                    project(0, a)
+                rope_tables()
+                cast(4)
+                load_w(5)
+            for a in range(2):
+                project(ip - 2, a)
             if ip == 11:
                 norm_a(0)
-            if ip == 12:
-                emit_parked(0)
-            if ip == 13:
-                emit_parked(4)
+            if ip in (13, 14, 15, 16):
+                emit_parked(0 if ip < 15 else 4, 2 * ((ip - 1) % 2), False)
+                emit_parked(0 if ip < 15 else 4, 2 * ((ip - 1) % 2) + 1, True)
         quantize(NPAIR - 1)
         for j in (2, 3):
             sumsq(2, j)
-        sine(NPAIR - 3)
-        cosine(NPAIR - 3, nc.gpsimd)
+        for j in (2, 3):
+            emit(12, 4, j, False)
         for a in range(2):
             project(NPAIR - 1, a)
         for j in range(TT):
             sumsq(3, j)
-        sine(NPAIR - 2)
-        cosine(NPAIR - 2, nc.vector)
         for j in range(TT):
             sumsq(4, j)
         norm_a(1)
         norm_b(1)
-        sine(NPAIR - 1)
-        cosine(NPAIR - 1, nc.vector)
-        for h0 in (16, 20, 24, 28):
+        work_list = []
+        for h0 in (16, 20):
             for j in range(TT):
-                emit(h0, 4, j, j % 2 == 1)
+                work_list.append((flush_scalar, back, h0, j))
+                work_list.append((rope_tokens, turn_y, h0 + 8, j))
+        banks = {}
+        for i in range(len(work_list) + 5):
+            if i < len(work_list):
+                finish, start, h0, j = work_list[i]
+                banks[i] = start(h0, j) if start is turn_y else start(h0, 4, j)
+            if i >= 5:
+                finish, start, h0, j = work_list[i - 5]
+                finish(h0, j, banks[i - 5])

@@ -309,14 +309,15 @@ def tile_dynamicselfattention_pa_kernel(
             if r >= 3:
                 if j == TT - 1:
                     nc.vector.reduce_sum(out=part[:, r, :], in_=ssb[:], axis=mybir.AxisListType.X)
-            else:
-                junk = work.tile([P, HD], F32, name="junk")
-                nc.scalar.activation(
-                    out=junk[:],
-                    in_=ssb[:, j, :],
-                    func=ACT.Copy,
-                    accum_out=part[:, r, j : j + 1],
-                )
+            elif j == TT - 1:
+                for i in range(TT):
+                    junk = work.tile([P, HD], F32, name="junk")
+                    nc.scalar.activation(
+                        out=junk[:],
+                        in_=ssb[:, i, :],
+                        func=ACT.Copy,
+                        accum_out=part[:, r, i : i + 1],
+                    )
 
         def norm_a(qk):
             rounds = slice(0, 2) if qk == 0 else slice(2, 5)

@@ -21,7 +21,7 @@ NPAIR = NH // 2
 PASSES = 4
 TT = 4
 EPS = 1e-6
-G_CAST = 1536
+G_CAST = 1600
 FLOPS = 2 * S * 2 * DIM * DIM
 
 
@@ -53,8 +53,9 @@ def tile_dynamicselfattention_pa_kernel(
             wb_tiles[c] = wbytes
 
         wb_tiles[0] = wbp.tile([P, 2, DIM], U8, name="wbytes")
-        nc.sync.dma_start(out=wb_tiles[0][:, 0, :], in_=w_view[0][:, 0, :])
-        nc.sync.dma_start(out=wb_tiles[0][:, 1, :], in_=w_view[0][:, 1, :])
+        for half in range(2):
+            k_half = slice(half * DIM // 2, (half + 1) * DIM // 2)
+            nc.sync.dma_start(out=wb_tiles[0][:, :, k_half], in_=w_view[0][:, :, k_half])
         scale_t = const.tile([P, PASSES, 1, 4], F32, name="scale_t")
         nc.scalar.dma_start(
             out=scale_t[:].rearrange("p g o t -> p (g o) t"),
@@ -179,7 +180,7 @@ def tile_dynamicselfattention_pa_kernel(
         st = {}
 
         def sorted_head(ip):
-            return ip >= 5 and ip % 2 == 1
+            return ip >= 7 and ip % 2 == 1
 
         def cast(ip):
             wide = widep.tile([P, 2 * DIM], BF16, name="wide")
@@ -187,9 +188,12 @@ def tile_dynamicselfattention_pa_kernel(
             wb = wb_tiles[ip][:].rearrange("p a k -> p (a k)")
             if ip == 0:
                 shares = (
-                    (0, DIM, nc.vector.tensor_copy),
-                    (DIM, DIM + DIM // 2, nc.scalar.copy),
-                    (DIM + DIM // 2, 2 * DIM, nc.gpsimd.tensor_copy),
+                    (0, 1024, nc.vector.tensor_copy),
+                    (2048, 2560, nc.scalar.copy),
+                    (2560, 3072, nc.gpsimd.tensor_copy),
+                    (1024, 2048, nc.vector.tensor_copy),
+                    (3072, 3584, nc.scalar.copy),
+                    (3584, 4096, nc.gpsimd.tensor_copy),
                 )
             elif ip <= 2:
                 shares = ((0, DIM, nc.gpsimd.tensor_copy), (DIM, 2 * DIM, nc.scalar.copy))
@@ -242,19 +246,27 @@ def tile_dynamicselfattention_pa_kernel(
                 op=ALU.mult,
             )
 
-        def quantize(ip):
-            codes = codep.tile([P, 2 * PASSES * P], U32, name="codes", align_bytes=64)
-            wsc = codep.tile([P, 2 * PASSES * P], U8, name="wsc", align_bytes=64)
+        def quantize(ip, lo=0, hi=PASSES):
+            if lo == 0:
+                st[("codes", ip)] = (
+                    codep.tile([P, 2 * PASSES * P], U32, name="codes", align_bytes=64),
+                    codep.tile([P, 2 * PASSES * P], U8, name="wsc", align_bytes=64),
+                )
+            codes, wsc = st[("codes", ip)]
+            cols = slice(lo * 2 * P, hi * 2 * P)
             nc.vector.quantize_mx(
-                out=codes[:].bitcast(FP8X4), scales=wsc[:], in_=st[("grouped", ip)][:]
+                out=codes[:, cols].bitcast(FP8X4),
+                scales=wsc[:, cols],
+                in_=st[("grouped", ip)][:, lo * 8 * P : hi * 8 * P],
             )
-            st[("codes", ip)] = (codes, wsc)
 
-        def project(ip, a):
+        def project(ip, a, lo=0, hi=PASSES):
             codes, wsc = st[("codes", ip)]
             h = 2 * ip + a
-            acc = psum.tile([P, S], F32, name="acc", tag="bank")
-            for g in range(PASSES):
+            if lo == 0:
+                st[("acc", h)] = psum.tile([P, S], F32, name="acc", tag="bank")
+            acc = st[("acc", h)]
+            for g in range(lo, hi):
                 cols = slice((2 * g + a) * P, (2 * g + a + 1) * P)
                 nc.tensor.matmul_mx(
                     out=acc[:],
@@ -265,28 +277,24 @@ def tile_dynamicselfattention_pa_kernel(
                     start=(g == 0),
                     stop=(g == PASSES - 1),
                 )
+            if hi < PASSES:
+                return
             sq = sqp.tile([P, S], F32, name="sq")
             nc.scalar.activation(
                 out=sq[:], in_=acc[:], func=ACT.Square, bias=bcol[:, h : h + 1], scale=1.0
             )
             st[("sq", h)] = sq
-            if ip == NPAIR - 1:
-                nc.vector.tensor_scalar(
-                    out=y_all[:, h, :],
-                    in0=acc[:],
-                    scalar1=gcol[:, h : h + 1],
-                    scalar2=bgcol[:, h : h + 1],
-                    op0=ALU.mult,
-                    op1=ALU.add,
-                )
-            else:
-                nc.scalar.activation(
-                    out=y_all[:, h, :],
-                    in_=acc[:],
-                    func=ACT.Identity,
-                    bias=bgcol[:, h : h + 1],
-                    scale=gcol[:, h : h + 1],
-                )
+            if ip < NPAIR - 1:
+                leave(h)
+
+        def leave(h):
+            nc.scalar.activation(
+                out=y_all[:, h, :],
+                in_=st[("acc", h)][:],
+                func=ACT.Identity,
+                bias=bgcol[:, h : h + 1],
+                scale=gcol[:, h : h + 1],
+            )
 
         ROUNDS = ((0, 8), (8, 16), (16, 24), (24, 30), (30, 32))
 
@@ -381,9 +389,6 @@ def tile_dynamicselfattention_pa_kernel(
         def emit(h0, n, j, on_vector):
             flush(h0, n, j, on_vector, back(h0, n, j))
 
-        def flush_scalar(h0, j, ob):
-            flush(h0, 4, j, False, ob)
-
         def flush(h0, n, j, on_vector, ob):
             scale = rstd[h0 // 16][:, j : j + 1]
             obuf = obp.tile([P, 4, HD], F32, name="obuf")
@@ -407,15 +412,17 @@ def tile_dynamicselfattention_pa_kernel(
                 nc.tensor.transpose(ob[:, hh, :], y_all[:, h0 + hh, j * P : (j + 1) * P], ident[:])
             return ob
 
+        tables = set()
+
         def rope_tokens(h0, j, ob):
-            if h0 == 24:
+            if j not in tables:
+                tables.add(j)
                 for src_t, dst_t in ((cos_t, cosn), (sinsg, sinn)):
-                    nc.vector.tensor_scalar(
+                    nc.scalar.activation(
                         out=dst_t[:, j, :],
-                        in0=src_t[:, j, :],
-                        scalar1=rstd[1][:, j : j + 1],
-                        scalar2=None,
-                        op0=ALU.mult,
+                        in_=src_t[:, j, :],
+                        func=ACT.Copy,
+                        scale=rstd[1][:, j : j + 1],
                     )
             ta = obp.tile([P, 4, HD], F32, name="obuf")
             tz = tokp.tile([P, 4, HD], F32, name="tz")
@@ -434,8 +441,39 @@ def tile_dynamicselfattention_pa_kernel(
                 .rearrange("p h (b d) -> p h b d", b=2),
                 op=ALU.mult,
             )
-            adder = nc.vector if h0 == 28 and j >= 2 else nc.gpsimd
+            adder = nc.vector if h0 == 28 and j >= 3 else nc.gpsimd
             adder.tensor_tensor(out=ta[:], in0=ta[:], in1=tz[:], op=ALU.add)
+            store(h0, 4, j, ta[:].rearrange("p h d -> p (h d)"))
+
+        def rope_tokens_early(h0, j, ob):
+            ta = obp.tile([P, 4, HD], F32, name="obuf")
+            tz = tokp.tile([P, 4, HD], F32, name="tz")
+            nc.vector.tensor_tensor(
+                out=ta[:],
+                in0=ob[:],
+                in1=cos_t[:, j : j + 1, :].to_broadcast([P, 4, HD]),
+                op=ALU.mult,
+            )
+            nc.vector.tensor_tensor(
+                out=tz[:].rearrange("p h (b d) -> p h b d", b=2),
+                in0=ob[:].rearrange("p h (b d) -> p h b d", b=2)[:, :, ::-1, :],
+                in1=sinsg[:, j : j + 1, :]
+                .to_broadcast([P, 4, HD])
+                .rearrange("p h (b d) -> p h b d", b=2),
+                op=ALU.mult,
+            )
+            nc.gpsimd.tensor_tensor(out=ta[:], in0=ta[:], in1=tz[:], op=ALU.add)
+            st[("ta", h0, j)] = ta
+
+        def finish_early(h0, j):
+            ta = st[("ta", h0, j)]
+            nc.vector.tensor_scalar(
+                out=ta[:],
+                in0=ta[:],
+                scalar1=rstd[h0 // 16][:, j : j + 1],
+                scalar2=None,
+                op0=ALU.mult,
+            )
             store(h0, 4, j, ta[:].rearrange("p h d -> p (h d)"))
 
         PLACE = {0: 28, 4: 0}
@@ -511,6 +549,8 @@ def tile_dynamicselfattention_pa_kernel(
                     load_w(c + 1)
             for g in range(PASSES):
                 turn(ip - 1, g)
+                if ip == NPAIR and g == 2:
+                    quantize(NPAIR - 1, 0, 2)
             for x in EXTRAS.get(ip, []):
                 x[0](*x[1:])
             if ip == 3:
@@ -526,29 +566,37 @@ def tile_dynamicselfattention_pa_kernel(
             if ip in (13, 14, 15, 16):
                 emit_parked(0 if ip < 15 else 4, 2 * ((ip - 1) % 2), False)
                 emit_parked(0 if ip < 15 else 4, 2 * ((ip - 1) % 2) + 1, True)
-        quantize(NPAIR - 1)
-        for j in (2, 3):
-            sumsq(2, j)
-        for j in (2, 3):
-            emit(12, 4, j, False)
+        quantize(NPAIR - 1, 2, 4)
+        sumsq(2, 2)
+        sumsq(2, 3)
         for a in range(2):
-            project(NPAIR - 1, a)
-        for j in range(TT):
-            sumsq(3, j)
+            project(NPAIR - 1, a, 0, 2)
+        rope_tokens_early(24, 0, turn_y(24, 0))
+        sumsq(3, 0)
+        sumsq(3, 1)
+        for a in range(2):
+            project(NPAIR - 1, a, 2, 4)
+        for a in range(2):
+            leave(NH - 2 + a)
+        for j in (1, 2):
+            rope_tokens_early(24, j, turn_y(24, j))
+        sumsq(3, 2)
+        sumsq(3, 3)
         for j in range(TT):
             sumsq(4, j)
         norm_a(1)
         norm_b(1)
-        work_list = []
-        for h0 in (16, 20):
-            for j in range(TT):
-                work_list.append((flush_scalar, back, h0, j))
-                work_list.append((rope_tokens, turn_y, h0 + 8, j))
+        for j in range(3):
+            finish_early(24, j)
+        order = [(12, 2), (12, 3), (16, 0), (24, 3), (16, 1), (28, 0), (16, 2), (28, 1), (16, 3), (28, 2), (20, 0), (28, 3), (20, 1), (20, 2), (20, 3)]
         banks = {}
-        for i in range(len(work_list) + 5):
-            if i < len(work_list):
-                finish, start, h0, j = work_list[i]
-                banks[i] = start(h0, j) if start is turn_y else start(h0, 4, j)
+        for i in range(len(order) + 5):
+            if i < len(order):
+                h0, j = order[i]
+                banks[i] = turn_y(h0, j) if h0 >= 24 else back(h0, 4, j)
             if i >= 5:
-                finish, start, h0, j = work_list[i - 5]
-                finish(h0, j, banks[i - 5])
+                h0, j = order[i - 5]
+                if h0 >= 24:
+                    rope_tokens(h0, j, banks[i - 5])
+                else:
+                    flush(h0, 4, j, False, banks[i - 5])

@@ -21,7 +21,7 @@ NPAIR = NH // 2
 PASSES = 4
 TT = 4
 EPS = 1e-6
-G_CAST = 1600
+G_CAST = 1088
 FLOPS = 2 * S * 2 * DIM * DIM
 
 
@@ -158,18 +158,16 @@ def tile_dynamicselfattention_pa_kernel(
             )
 
         def token_table():
-            nc.vector.tensor_scalar(
-                out=sinsg[:, :, 0:64],
-                in0=sin_t[:, :, 0:64],
-                scalar1=-1.0,
-                scalar2=None,
-                op0=ALU.mult,
-            )
-            nc.vector.tensor_copy(out=sinsg[:, :, 64:128], in_=sin_t[:, :, 64:128])
+            nc.gpsimd.tensor_copy(out=sinsg[:, :, 0:64], in_=sinsw[:, :, 64:128])
+            nc.gpsimd.tensor_copy(out=sinsg[:, :, 64:128], in_=sinsw[:, :, 0:64])
 
         def rope_tables():
             for src_t, dst_t in ((cos_t, cosT), (sinsw, sinT)):
-                tb = psum.tile([P, S], BF16, name="tb", tag="bank")
+                if src_t is cos_t:
+                    tb = psum.tile([P, S], BF16, name="tb", tag="bank")
+                else:
+                    tb = psum1.tile([P, S], BF16, name="tb1")
+                    st["tb"] = tb
                 for j in range(TT):
                     nc.tensor.transpose(tb[:, j * P : (j + 1) * P], src_t[:, j, :], ident_bf[:])
                 nc.scalar.copy(out=dst_t[:, 0, :], in_=tb[:])
@@ -180,7 +178,7 @@ def tile_dynamicselfattention_pa_kernel(
         st = {}
 
         def sorted_head(ip):
-            return ip >= 7 and ip % 2 == 1
+            return False
 
         def cast(ip):
             wide = widep.tile([P, 2 * DIM], BF16, name="wide")
@@ -197,25 +195,27 @@ def tile_dynamicselfattention_pa_kernel(
                 )
             elif ip <= 2:
                 shares = ((0, DIM, nc.gpsimd.tensor_copy), (DIM, 2 * DIM, nc.scalar.copy))
-            elif ip <= 4:
-                shares = ((0, DIM, nc.scalar.copy), (DIM, 2 * DIM, nc.scalar.copy))
             else:
+                cut = 2 * DIM - (1280 if ip == 4 else G_CAST)
                 shares = (
                     (0, DIM, nc.scalar.copy),
-                    (DIM, 2 * DIM - G_CAST, nc.scalar.copy),
-                    (2 * DIM - G_CAST, 2 * DIM, nc.gpsimd.tensor_copy),
+                    (DIM, cut, nc.scalar.copy),
+                    (cut, 2 * DIM, nc.gpsimd.tensor_copy),
                 )
             for lo, hi, copy in shares:
                 copy(out=wide[:, lo:hi], in_=wb[:, lo:hi].bitcast(FP8))
             if sorted_head(ip):
-                sw = work.tile([P, DIM // 2], F32, name="sw")
-                nc.scalar.copy(
-                    out=sw[:].rearrange("p (g u q) -> p g u q", g=PASSES, u=2),
-                    in_=wide[:, 0:DIM]
-                    .bitcast(F32)
-                    .rearrange("p (g q u) -> p g u q", g=PASSES, u=2),
-                )
-                st[("sw", ip)] = sw
+                sort_words(ip, 0)
+
+        def sort_words(ip, a):
+            sw = work.tile([P, DIM // 2], F32, name="sw")
+            nc.scalar.copy(
+                out=sw[:].rearrange("p (g u q) -> p g u q", g=PASSES, u=2),
+                in_=st[("wide", ip)][:, a * DIM : (a + 1) * DIM]
+                .bitcast(F32)
+                .rearrange("p (g q u) -> p g u q", g=PASSES, u=2),
+            )
+            st[("sw", ip, a)] = sw
 
         def turn(ip, g):
             if g == 0:
@@ -231,8 +231,9 @@ def tile_dynamicselfattention_pa_kernel(
                 for u in range(2):
                     w0 = a * (DIM // 2) + 256 * g
                     src = words[:, w0 + u : w0 + 256 : 2]
-                    if a == 0 and sorted_head(ip):
-                        src = st[("sw", ip)][:, w0 + u * P : w0 + (u + 1) * P]
+                    if ("sw", ip, a) in st:
+                        v0 = 256 * g + u * P
+                        src = st[("sw", ip, a)][:, v0 : v0 + P]
                     nc.tensor.transpose(xt[:, u, a, :], src, ident[:])
             nc.vector.tensor_tensor(
                 out=gv[:, g, :, :, :],
@@ -298,34 +299,23 @@ def tile_dynamicselfattention_pa_kernel(
 
         ROUNDS = ((0, 8), (8, 16), (16, 24), (24, 30), (30, 32))
 
-        def sumsq(r, j):
+        def sumsq(r, half):
             lo, hi = ROUNDS[r]
-            if j == 0 and r < 4:
-                st[("ssb", r)] = psum1.tile([P, TT, HD], F32, name="ssb")
-            elif j == 0:
-                st[("ssb", r)] = psum.tile([P, TT, HD], F32, name="ssb2", tag="bank")
-            ssb = st[("ssb", r)]
-            for h in range(lo, hi):
-                nc.tensor.matmul(
-                    out=ssb[:, j, :],
-                    lhsT=st[("sq", h)][:, j * P : (j + 1) * P],
-                    rhs=ident[:],
-                    start=(h == lo),
-                    stop=(h == hi - 1),
-                    is_transpose=True,
-                )
-            if r >= 3:
-                if j == TT - 1:
-                    nc.vector.reduce_sum(out=part[:, r, :], in_=ssb[:], axis=mybir.AxisListType.X)
-            elif j == TT - 1:
-                for i in range(TT):
-                    junk = work.tile([P, HD], F32, name="junk")
-                    nc.scalar.activation(
-                        out=junk[:],
-                        in_=ssb[:, i, :],
-                        func=ACT.Copy,
-                        accum_out=part[:, r, i : i + 1],
+            j0 = 2 * half
+            ssb = psum.tile([P, 2, HD], F32, name="ssb", tag="bank")
+            for i in range(2):
+                for h in range(lo, hi):
+                    nc.tensor.matmul(
+                        out=ssb[:, i, :],
+                        lhsT=st[("sq", h)][:, (j0 + i) * P : (j0 + i + 1) * P],
+                        rhs=ident[:],
+                        start=(h == lo),
+                        stop=(h == hi - 1),
+                        is_transpose=True,
                     )
+            nc.vector.reduce_sum(
+                out=part[:, r, j0 : j0 + 2], in_=ssb[:], axis=mybir.AxisListType.X
+            )
 
         def norm_a(qk):
             rounds = slice(0, 2) if qk == 0 else slice(2, 5)
@@ -344,19 +334,21 @@ def tile_dynamicselfattention_pa_kernel(
         def norm_b(qk):
             nc.vector.reciprocal(out=rstd[qk][:], in_=st[("rms", qk)][:])
 
-        def sine(ip):
+        def rope_a(ip):
             z = zp.tile([P, 2, S], F32, name="z")
             nc.vector.tensor_tensor(
-                out=z[:],
-                in0=y_all[:, 2 * ip : 2 * ip + 2, :],
-                in1=sinT[:].to_broadcast([P, 2, S]),
-                op=ALU.mult,
+                out=z[:, 0, :], in0=y_all[:, 2 * ip, :], in1=st["tb"][:], op=ALU.mult
             )
             st[("z", ip)] = z
 
-        def cosine(ip, eng):
-            y = y_all[:, 2 * ip : 2 * ip + 2, :]
-            eng.tensor_tensor(out=y, in0=y, in1=cosT[:].to_broadcast([P, 2, S]), op=ALU.mult)
+        def rope_b(ip):
+            z = st[("z", ip)]
+            mul = nc.gpsimd.tensor_tensor
+            ya = y_all[:, 2 * ip, :]
+            yb = y_all[:, 2 * ip + 1, :]
+            mul(out=ya, in0=ya, in1=cosT[:, 0, :], op=ALU.mult)
+            mul(out=z[:, 1, :], in0=yb, in1=sinT[:, 0, :], op=ALU.mult)
+            mul(out=yb, in0=yb, in1=cosT[:, 0, :], op=ALU.mult)
 
         def back(h0, n, j):
             ob = psum.tile([P, 4, HD], F32, name="ob", tag="bank")
@@ -497,16 +489,16 @@ def tile_dynamicselfattention_pa_kernel(
 
         EXTRAS = {
             6: [(park, 0, 0), (park, 0, 1)],
-            7: [(sumsq, 0, 0), (sumsq, 0, 1), (park, 0, 2)],
-            8: [(sumsq, 0, 2), (sumsq, 0, 3)],
+            7: [(sumsq, 0, 0), (park, 0, 2)],
+            8: [(sumsq, 0, 1)],
             9: [(park, 0, 3), (park, 4, 0)],
-            10: [(sumsq, 1, 0), (sumsq, 1, 1), (sumsq, 1, 2)],
-            11: [(sumsq, 1, 3), (park, 4, 1)],
+            10: [(sumsq, 1, 0), (park, 4, 1)],
+            11: [(sumsq, 1, 1)],
             12: [(park, 4, 2), (park, 4, 3)],
-            13: [(emit, 8, 4, 0, False), (emit, 8, 4, 1, False)],
-            14: [(emit, 8, 4, 2, False), (emit, 8, 4, 3, False)],
-            15: [(emit, 12, 4, 0, False), (emit, 12, 4, 1, False), (sumsq, 2, 0)],
-            16: [(sumsq, 2, 1)],
+            13: [(emit, 8, 4, 0, False), (emit, 8, 4, 1, True)],
+            14: [(emit, 8, 4, 2, False), (emit, 8, 4, 3, True)],
+            15: [(emit, 12, 4, 0, False), (emit, 12, 4, 1, True)],
+            16: [(sumsq, 2, 0)],
         }
         ctx.enter_context(
             tc.manual_schedule(
@@ -532,16 +524,18 @@ def tile_dynamicselfattention_pa_kernel(
         quantize(0)
         columns()
         for ip in range(3, NPAIR + 1):
+            if 4 <= ip < 16:
+                rope_a(ip - 4)
             quantize(ip - 2)
             if ip == 3:
                 small_vector_work()
+                token_table()
             if ip == 13:
                 norm_b(0)
-            if ip == 9:
-                token_table()
             if 4 <= ip < 16:
-                sine(ip - 4)
-                cosine(ip - 4, nc.gpsimd)
+                rope_b(ip - 4)
+            if ip == NPAIR - 1:
+                sort_words(ip, 1)
             c = 3 if ip == 3 else ip + 1
             if c < NPAIR:
                 cast(c)
@@ -565,30 +559,26 @@ def tile_dynamicselfattention_pa_kernel(
                 norm_a(0)
             if ip in (13, 14, 15, 16):
                 emit_parked(0 if ip < 15 else 4, 2 * ((ip - 1) % 2), False)
-                emit_parked(0 if ip < 15 else 4, 2 * ((ip - 1) % 2) + 1, True)
+                emit_parked(0 if ip < 15 else 4, 2 * ((ip - 1) % 2) + 1, False)
         quantize(NPAIR - 1, 2, 4)
-        sumsq(2, 2)
-        sumsq(2, 3)
+        sumsq(2, 1)
         for a in range(2):
             project(NPAIR - 1, a, 0, 2)
         rope_tokens_early(24, 0, turn_y(24, 0))
         sumsq(3, 0)
-        sumsq(3, 1)
         for a in range(2):
             project(NPAIR - 1, a, 2, 4)
         for a in range(2):
             leave(NH - 2 + a)
-        for j in (1, 2):
-            rope_tokens_early(24, j, turn_y(24, j))
-        sumsq(3, 2)
-        sumsq(3, 3)
-        for j in range(TT):
-            sumsq(4, j)
+        rope_tokens_early(24, 1, turn_y(24, 1))
+        sumsq(3, 1)
+        sumsq(4, 0)
+        sumsq(4, 1)
         norm_a(1)
         norm_b(1)
-        for j in range(3):
+        for j in range(2):
             finish_early(24, j)
-        order = [(12, 2), (12, 3), (16, 0), (24, 3), (16, 1), (28, 0), (16, 2), (28, 1), (16, 3), (28, 2), (20, 0), (28, 3), (20, 1), (20, 2), (20, 3)]
+        order = [(12, 2), (12, 3), (16, 0), (24, 2), (16, 1), (24, 3), (16, 2), (28, 0), (16, 3), (28, 1), (20, 0), (28, 2), (20, 1), (28, 3), (20, 2), (20, 3)]
         banks = {}
         for i in range(len(order) + 5):
             if i < len(order):

from contextlib import ExitStack

import concourse.mybir as mybir
from concourse.masks import make_identity

F32 = mybir.dt.float32
BF16 = mybir.dt.bfloat16
U32 = mybir.dt.uint32
U8 = mybir.dt.uint8
FP8 = mybir.dt.float8_e4m3fn
FP8X4 = mybir.dt.float8_e4m3fn_x4
ALU = mybir.AluOpType
ACT = mybir.ActivationFunctionType

P = 128
S = 512
DIM = 2048
HD = 128
NH = 32
NPAIR = NH // 2
PASSES = 4
TT = 4
EPS = 1e-6
G_CAST = 1088
FLOPS = 2 * S * 2 * DIM * DIM


def tile_dynamicselfattention_pa_kernel(
    tc, hidden_states, cos, sin, w_qk_bytes, w_qk_scale, b_qk, g_q, g_k, out_0, out_1
):
    nc = tc.nc
    outs = (out_0, out_1)
    with ExitStack() as ctx:
        const = ctx.enter_context(tc.tile_pool(name="const", bufs=1))
        big = ctx.enter_context(tc.tile_pool(name="big", bufs=1))
        wbp = ctx.enter_context(tc.tile_pool(name="wbp", bufs=3))
        widep = ctx.enter_context(tc.tile_pool(name="widep", bufs=3))
        work = ctx.enter_context(tc.tile_pool(name="work", bufs=2))
        codep = ctx.enter_context(tc.tile_pool(name="codep", bufs=2))
        sqp = ctx.enter_context(tc.tile_pool(name="sqp", bufs=14))
        zp = ctx.enter_context(tc.tile_pool(name="zp", bufs=7))
        tokp = ctx.enter_context(tc.tile_pool(name="tokp", bufs=3))
        obp = ctx.enter_context(tc.tile_pool(name="obp", bufs=10))
        psum = ctx.enter_context(tc.psum_pool(name="psum", bufs=7))
        psum1 = ctx.enter_context(tc.psum_pool(name="psum1", bufs=1))

        w_view = w_qk_bytes.rearrange("(c a p) k -> c p a k", a=2, p=P)
        wb_tiles = {}

        def load_w(c):
            wbytes = wbp.tile([P, 2, DIM], U8, name="wbytes")
            nc.sync.dma_start(out=wbytes[:], in_=w_view[c])
            wb_tiles[c] = wbytes

        wb_tiles[0] = wbp.tile([P, 2, DIM], U8, name="wbytes")
        for half in range(2):
            k_half = slice(half * DIM // 2, (half + 1) * DIM // 2)
            nc.sync.dma_start(out=wb_tiles[0][:, :, k_half], in_=w_view[0][:, :, k_half])
        scale_t = const.tile([P, PASSES, 1, 4], F32, name="scale_t")
        nc.scalar.dma_start(
            out=scale_t[:].rearrange("p g o t -> p (g o) t"),
            in_=w_qk_scale.rearrange("o (g p t) -> p (o g) t", p=P, t=4),
        )
        load_w(1)
        hs_view = hidden_states.rearrange("o (j p) k -> (o j) p k", p=P)
        hs_tiles = []
        for j in range(TT):
            hs_t = big.tile(
                [P, DIM], BF16, name="hs_t%d" % j, offset=16384 + 4096 * j, align_bytes=64
            )
            nc.sync.dma_start(out=hs_t[:], in_=hs_view[j])
            hs_tiles.append(hs_t)

        vecs = const.tile([P, P], BF16, name="vecs")
        nc.gpsimd.memset(vecs[:], 0.0)
        nc.sync.dma_start(out=vecs[0:32, :], in_=b_qk.rearrange("(h d) -> h d", d=HD))
        nc.sync.dma_start(out=vecs[32:48, :], in_=g_q.rearrange("(h d) -> h d", d=HD))
        nc.sync.dma_start(out=vecs[48:64, :], in_=g_k.rearrange("(h d) -> h d", d=HD))
        cos_t = const.tile([P, TT, HD], BF16, name="cos_t")
        sin_t = const.tile([P, TT, HD], BF16, name="sin_t")
        nc.sync.dma_start(out=cos_t[:], in_=cos.rearrange("(j p) d -> p j d", p=P))
        nc.sync.dma_start(out=sin_t[:], in_=sin.rearrange("(j p) d -> p j d", p=P))
        load_w(2)

        eps_t = const.tile([P, 1], F32, name="eps_t")
        nc.gpsimd.memset(eps_t[:], EPS)
        warm = const.tile([P, 1], F32, name="warm")
        nc.vector.memset(warm[:], 0.0)
        nc.scalar.activation(out=warm[:], in_=warm[:], func=ACT.Square)

        ident = const.tile([P, P], F32, name="ident")
        make_identity(nc, ident[:])
        ident_bf = const.tile([P, P], BF16, name="ident_bf")
        make_identity(nc, ident_bf[:])
        perm = const.tile([P, P], F32, name="perm")
        nc.gpsimd.tensor_copy(out=perm[:, 0:64], in_=ident[:, 64:128])
        nc.gpsimd.tensor_copy(out=perm[:, 64:128], in_=ident[:, 0:64])

        hgr = big.tile([P, PASSES * S * 4], BF16, name="hgr", offset=0, align_bytes=64)
        hgr_w = hgr[:].bitcast(F32).rearrange("p (g s u) -> p g s u", g=PASSES, u=2)
        hs_codes = const.tile([P, PASSES * S], U32, name="hs_codes", align_bytes=64)
        hs_sc = const.tile([P, PASSES * S], U8, name="hs_sc", align_bytes=64)

        def turn_hidden(tiles):
            for j in tiles:
                words = hs_tiles[j][:].bitcast(F32)
                for b in range(2):
                    xt = psum.tile([P, 512], F32, name="xt", tag="bank")
                    for gg in range(2):
                        for u in range(2):
                            g = 2 * b + gg
                            c0 = (gg * 2 + u) * P
                            nc.tensor.transpose(
                                xt[:, c0 : c0 + P],
                                words[:, 256 * g + u : 256 * (g + 1) : 2],
                                ident[:],
                            )
                    nc.scalar.copy(
                        out=hgr_w[:, 2 * b : 2 * b + 2, j * P : (j + 1) * P, :],
                        in_=xt[:].rearrange("p (g u n) -> p g n u", g=2, u=2),
                    )

        def quantize_hidden():
            for c in range(2):
                nc.vector.quantize_mx(
                    out=hs_codes[:, c * 1024 : (c + 1) * 1024].bitcast(FP8X4),
                    scales=hs_sc[:, c * 1024 : (c + 1) * 1024],
                    in_=hgr[:, c * 4096 : (c + 1) * 4096],
                )

        bcol = const.tile([P, NH], F32, name="bcol")
        gcol = const.tile([P, NH], F32, name="gcol")
        bgcol = const.tile([P, NH], F32, name="bgcol")

        def columns():
            vt = psum.tile([P, P], BF16, name="vt", tag="bank")
            nc.tensor.transpose(vt[:], vecs[:], ident_bf[:])
            nc.scalar.copy(out=bcol[:], in_=vt[:, 0:32])
            nc.scalar.copy(out=gcol[:], in_=vt[:, 32:64])

        cosT = const.tile([P, 1, S], BF16, name="cosT")
        sinT = const.tile([P, 1, S], BF16, name="sinT")

        sinsw = const.tile([P, TT, HD], BF16, name="sinsw")
        sinsg = const.tile([P, TT, HD], BF16, name="sinsg")
        cosn = const.tile([P, TT, HD], F32, name="cosn")
        sinn = const.tile([P, TT, HD], F32, name="sinn")

        def small_vector_work():
            nc.vector.tensor_tensor(out=bgcol[:], in0=bcol[:], in1=gcol[:], op=ALU.mult)
            nc.vector.tensor_copy(out=sinsw[:, :, 0:64], in_=sin_t[:, :, 64:128])
            nc.vector.tensor_scalar(
                out=sinsw[:, :, 64:128],
                in0=sin_t[:, :, 0:64],
                scalar1=-1.0,
                scalar2=None,
                op0=ALU.mult,
            )

        def token_table():
            nc.gpsimd.tensor_copy(out=sinsg[:, :, 0:64], in_=sinsw[:, :, 64:128])
            nc.gpsimd.tensor_copy(out=sinsg[:, :, 64:128], in_=sinsw[:, :, 0:64])

        def rope_tables():
            for src_t, dst_t in ((cos_t, cosT), (sinsw, sinT)):
                if src_t is cos_t:
                    tb = psum.tile([P, S], BF16, name="tb", tag="bank")
                else:
                    tb = psum1.tile([P, S], BF16, name="tb1")
                    st["tb"] = tb
                for j in range(TT):
                    nc.tensor.transpose(tb[:, j * P : (j + 1) * P], src_t[:, j, :], ident_bf[:])
                nc.scalar.copy(out=dst_t[:, 0, :], in_=tb[:])

        y_all = big.tile([P, NH, S], F32, name="y_all", offset=0, align_bytes=64)
        part = const.tile([P, 5, TT], F32, name="part")
        rstd = [const.tile([P, TT], F32, name="rstd%d" % i) for i in range(2)]
        st = {}

        def sorted_head(ip):
            return False

        def cast(ip):
            wide = widep.tile([P, 2 * DIM], BF16, name="wide")
            st[("wide", ip)] = wide
            wb = wb_tiles[ip][:].rearrange("p a k -> p (a k)")
            if ip == 0:
                shares = (
                    (0, 1024, nc.vector.tensor_copy),
                    (2048, 2560, nc.scalar.copy),
                    (2560, 3072, nc.gpsimd.tensor_copy),
                    (1024, 2048, nc.vector.tensor_copy),
                    (3072, 3584, nc.scalar.copy),
                    (3584, 4096, nc.gpsimd.tensor_copy),
                )
            elif ip <= 2:
                shares = ((0, DIM, nc.gpsimd.tensor_copy), (DIM, 2 * DIM, nc.scalar.copy))
            else:
                cut = 2 * DIM - (1280 if ip == 4 else G_CAST)
                shares = (
                    (0, DIM, nc.scalar.copy),
                    (DIM, cut, nc.scalar.copy),
                    (cut, 2 * DIM, nc.gpsimd.tensor_copy),
                )
            for lo, hi, copy in shares:
                copy(out=wide[:, lo:hi], in_=wb[:, lo:hi].bitcast(FP8))
            if sorted_head(ip):
                sort_words(ip, 0)

        def sort_words(ip, a):
            sw = work.tile([P, DIM // 2], F32, name="sw")
            nc.scalar.copy(
                out=sw[:].rearrange("p (g u q) -> p g u q", g=PASSES, u=2),
                in_=st[("wide", ip)][:, a * DIM : (a + 1) * DIM]
                .bitcast(F32)
                .rearrange("p (g q u) -> p g u q", g=PASSES, u=2),
            )
            st[("sw", ip, a)] = sw

        def turn(ip, g):
            if g == 0:
                st[("grouped", ip)] = work.tile(
                    [P, 2 * DIM], BF16, name="grouped", align_bytes=64
                )
            words = st[("wide", ip)][:].bitcast(F32)
            gv = st[("grouped", ip)][:].rearrange(
                "p (g m u e) -> p g m u e", g=PASSES, u=2, e=2
            )
            xt = psum.tile([P, 2, 2, P], F32, name="xt", tag="bank")
            for a in range(2):
                for u in range(2):
                    w0 = a * (DIM // 2) + 256 * g
                    src = words[:, w0 + u : w0 + 256 : 2]
                    if ("sw", ip, a) in st:
                        v0 = 256 * g + u * P
                        src = st[("sw", ip, a)][:, v0 : v0 + P]
                    nc.tensor.transpose(xt[:, u, a, :], src, ident[:])
            nc.vector.tensor_tensor(
                out=gv[:, g, :, :, :],
                in0=xt[:]
                .rearrange("p u a n -> p u (a n)")
                .bitcast(BF16)
                .rearrange("p u (m e) -> p m u e", e=2),
                in1=scale_t[:, g, :, :]
                .to_broadcast([P, 2 * P, 4])
                .rearrange("p m (u e) -> p m u e", e=2),
                op=ALU.mult,
            )

        def quantize(ip, lo=0, hi=PASSES):
            if lo == 0:
                st[("codes", ip)] = (
                    codep.tile([P, 2 * PASSES * P], U32, name="codes", align_bytes=64),
                    codep.tile([P, 2 * PASSES * P], U8, name="wsc", align_bytes=64),
                )
            codes, wsc = st[("codes", ip)]
            cols = slice(lo * 2 * P, hi * 2 * P)
            nc.vector.quantize_mx(
                out=codes[:, cols].bitcast(FP8X4),
                scales=wsc[:, cols],
                in_=st[("grouped", ip)][:, lo * 8 * P : hi * 8 * P],
            )

        def project(ip, a, lo=0, hi=PASSES):
            codes, wsc = st[("codes", ip)]
            h = 2 * ip + a
            if lo == 0:
                st[("acc", h)] = psum.tile([P, S], F32, name="acc", tag="bank")
            acc = st[("acc", h)]
            for g in range(lo, hi):
                cols = slice((2 * g + a) * P, (2 * g + a + 1) * P)
                nc.tensor.matmul_mx(
                    out=acc[:],
                    lhsT=codes[:, cols].bitcast(FP8X4),
                    lhsT_scale=wsc[:, cols],
                    rhs=hs_codes[:, g * S : (g + 1) * S].bitcast(FP8X4),
                    rhs_scale=hs_sc[:, g * S : (g + 1) * S],
                    start=(g == 0),
                    stop=(g == PASSES - 1),
                )
            if hi < PASSES:
                return
            sq = sqp.tile([P, S], F32, name="sq")
            nc.scalar.activation(
                out=sq[:], in_=acc[:], func=ACT.Square, bias=bcol[:, h : h + 1], scale=1.0
            )
            st[("sq", h)] = sq
            if ip < NPAIR - 1:
                leave(h)

        def leave(h):
            nc.scalar.activation(
                out=y_all[:, h, :],
                in_=st[("acc", h)][:],
                func=ACT.Identity,
                bias=bgcol[:, h : h + 1],
                scale=gcol[:, h : h + 1],
            )

        ROUNDS = ((0, 8), (8, 16), (16, 24), (24, 30), (30, 32))

        def sumsq(r, half):
            lo, hi = ROUNDS[r]
            j0 = 2 * half
            ssb = psum.tile([P, 2, HD], F32, name="ssb", tag="bank")
            for i in range(2):
                for h in range(lo, hi):
                    nc.tensor.matmul(
                        out=ssb[:, i, :],
                        lhsT=st[("sq", h)][:, (j0 + i) * P : (j0 + i + 1) * P],
                        rhs=ident[:],
                        start=(h == lo),
                        stop=(h == hi - 1),
                        is_transpose=True,
                    )
            nc.vector.reduce_sum(
                out=part[:, r, j0 : j0 + 2], in_=ssb[:], axis=mybir.AxisListType.X
            )

        def norm_a(qk):
            rounds = slice(0, 2) if qk == 0 else slice(2, 5)
            ssum = work.tile([P, TT], F32, name="ssum")
            nc.vector.reduce_sum(
                out=ssum[:],
                in_=part[:, rounds, :].rearrange("p r j -> p j r"),
                axis=mybir.AxisListType.X,
            )
            rms = work.tile([P, TT], F32, name="rms")
            nc.scalar.activation(
                out=rms[:], in_=ssum[:], func=ACT.Sqrt, bias=eps_t[:], scale=1.0 / DIM
            )
            st[("rms", qk)] = rms

        def norm_b(qk):
            nc.vector.reciprocal(out=rstd[qk][:], in_=st[("rms", qk)][:])

        def rope_a(ip):
            z = zp.tile([P, 2, S], F32, name="z")
            nc.vector.tensor_tensor(
                out=z[:, 0, :], in0=y_all[:, 2 * ip, :], in1=st["tb"][:], op=ALU.mult
            )
            st[("z", ip)] = z

        def rope_b(ip):
            z = st[("z", ip)]
            mul = nc.gpsimd.tensor_tensor
            ya = y_all[:, 2 * ip, :]
            yb = y_all[:, 2 * ip + 1, :]
            mul(out=ya, in0=ya, in1=cosT[:, 0, :], op=ALU.mult)
            mul(out=z[:, 1, :], in0=yb, in1=sinT[:, 0, :], op=ALU.mult)
            mul(out=yb, in0=yb, in1=cosT[:, 0, :], op=ALU.mult)

        def back(h0, n, j):
            ob = psum.tile([P, 4, HD], F32, name="ob", tag="bank")
            for hh in range(n):
                h = h0 + hh
                nc.tensor.matmul(
                    out=ob[:, hh, :],
                    lhsT=y_all[:, h, j * P : (j + 1) * P],
                    rhs=ident[:],
                    start=True,
                    stop=False,
                    is_transpose=True,
                )
                nc.tensor.matmul(
                    out=ob[:, hh, :],
                    lhsT=st[("z", h // 2)][:, h % 2, j * P : (j + 1) * P],
                    rhs=perm[:],
                    start=False,
                    stop=True,
                    is_transpose=True,
                )
            return ob

        def store(h0, n, j, src):
            qk = h0 // 16
            c0 = (h0 % 16) * HD
            dst = outs[qk].rearrange("o (j p) h d -> p (o j) (h d)", p=P)
            nc.sync.dma_start(out=dst[:, j, c0 : c0 + n * HD], in_=src)

        def emit(h0, n, j, on_vector):
            flush(h0, n, j, on_vector, back(h0, n, j))

        def flush(h0, n, j, on_vector, ob):
            scale = rstd[h0 // 16][:, j : j + 1]
            obuf = obp.tile([P, 4, HD], F32, name="obuf")
            if on_vector:
                nc.vector.tensor_scalar(
                    out=obuf[:, 0:n, :],
                    in0=ob[:, 0:n, :],
                    scalar1=scale,
                    scalar2=None,
                    op0=ALU.mult,
                )
            else:
                nc.scalar.activation(
                    out=obuf[:, 0:n, :], in_=ob[:, 0:n, :], func=ACT.Copy, scale=scale
                )
            store(h0, n, j, obuf[:, 0:n, :].rearrange("p h d -> p (h d)"))

        def turn_y(h0, j):
            ob = psum.tile([P, 4, HD], F32, name="ob", tag="bank")
            for hh in range(4):
                nc.tensor.transpose(ob[:, hh, :], y_all[:, h0 + hh, j * P : (j + 1) * P], ident[:])
            return ob

        tables = set()

        def rope_tokens(h0, j, ob):
            if j not in tables:
                tables.add(j)
                for src_t, dst_t in ((cos_t, cosn), (sinsg, sinn)):
                    nc.scalar.activation(
                        out=dst_t[:, j, :],
                        in_=src_t[:, j, :],
                        func=ACT.Copy,
                        scale=rstd[1][:, j : j + 1],
                    )
            ta = obp.tile([P, 4, HD], F32, name="obuf")
            tz = tokp.tile([P, 4, HD], F32, name="tz")
            nc.vector.tensor_tensor(
                out=ta[:],
                in0=ob[:],
                in1=cosn[:, j : j + 1, :].to_broadcast([P, 4, HD]),
                op=ALU.mult,
            )
            halves = ob[:].rearrange("p h (b d) -> p h b d", b=2)
            nc.vector.tensor_tensor(
                out=tz[:].rearrange("p h (b d) -> p h b d", b=2),
                in0=halves[:, :, ::-1, :],
                in1=sinn[:, j : j + 1, :]
                .to_broadcast([P, 4, HD])
                .rearrange("p h (b d) -> p h b d", b=2),
                op=ALU.mult,
            )
            adder = nc.vector if h0 == 28 and j >= 3 else nc.gpsimd
            adder.tensor_tensor(out=ta[:], in0=ta[:], in1=tz[:], op=ALU.add)
            store(h0, 4, j, ta[:].rearrange("p h d -> p (h d)"))

        def rope_tokens_early(h0, j, ob):
            ta = obp.tile([P, 4, HD], F32, name="obuf")
            tz = tokp.tile([P, 4, HD], F32, name="tz")
            nc.vector.tensor_tensor(
                out=ta[:],
                in0=ob[:],
                in1=cos_t[:, j : j + 1, :].to_broadcast([P, 4, HD]),
                op=ALU.mult,
            )
            nc.vector.tensor_tensor(
                out=tz[:].rearrange("p h (b d) -> p h b d", b=2),
                in0=ob[:].rearrange("p h (b d) -> p h b d", b=2)[:, :, ::-1, :],
                in1=sinsg[:, j : j + 1, :]
                .to_broadcast([P, 4, HD])
                .rearrange("p h (b d) -> p h b d", b=2),
                op=ALU.mult,
            )
            nc.gpsimd.tensor_tensor(out=ta[:], in0=ta[:], in1=tz[:], op=ALU.add)
            st[("ta", h0, j)] = ta

        def finish_early(h0, j):
            ta = st[("ta", h0, j)]
            nc.vector.tensor_scalar(
                out=ta[:],
                in0=ta[:],
                scalar1=rstd[h0 // 16][:, j : j + 1],
                scalar2=None,
                op0=ALU.mult,
            )
            store(h0, 4, j, ta[:].rearrange("p h d -> p (h d)"))

        PLACE = {0: 28, 4: 0}

        def park(h0, j):
            ob = back(h0, 4, j)
            nc.scalar.copy(
                out=y_all[:, PLACE[h0] + j, :], in_=ob[:].rearrange("p h d -> p (h d)")
            )

        def emit_parked(h0, j, on_vector):
            y = y_all[:, PLACE[h0] + j, :]
            scale = rstd[h0 // 16][:, j : j + 1]
            if on_vector:
                nc.vector.tensor_scalar(
                    out=y, in0=y, scalar1=scale, scalar2=None, op0=ALU.mult
                )
            else:
                nc.scalar.activation(out=y, in_=y, func=ACT.Copy, scale=scale)
            store(h0, 4, j, y)

        EXTRAS = {
            6: [(park, 0, 0), (park, 0, 1)],
            7: [(sumsq, 0, 0), (park, 0, 2)],
            8: [(sumsq, 0, 1)],
            9: [(park, 0, 3), (park, 4, 0)],
            10: [(sumsq, 1, 0), (park, 4, 1)],
            11: [(sumsq, 1, 1)],
            12: [(park, 4, 2), (park, 4, 3)],
            13: [(emit, 8, 4, 0, False), (emit, 8, 4, 1, True)],
            14: [(emit, 8, 4, 2, False), (emit, 8, 4, 3, True)],
            15: [(emit, 12, 4, 0, False), (emit, 12, 4, 1, True)],
            16: [(sumsq, 2, 0)],
        }
        ctx.enter_context(
            tc.manual_schedule(
                engines={
                    mybir.EngineType.PE,
                    mybir.EngineType.DVE,
                    mybir.EngineType.Pool,
                    mybir.EngineType.Activation,
                }
            )
        )
        cast(0)
        cast(1)
        for g in range(PASSES):
            turn(0, g)
        turn_hidden((0, 1))
        for g in range(PASSES):
            turn(1, g)
        turn_hidden((2, 3))
        cast(2)
        load_w(3)
        quantize_hidden()
        quantize(0)
        columns()
        for ip in range(3, NPAIR + 1):
            if 4 <= ip < 16:
                rope_a(ip - 4)
            quantize(ip - 2)
            if ip == 3:
                small_vector_work()
                token_table()
            if ip == 13:
                norm_b(0)
            if 4 <= ip < 16:
                rope_b(ip - 4)
            if ip == NPAIR - 1:
                sort_words(ip, 1)
            c = 3 if ip == 3 else ip + 1
            if c < NPAIR:
                cast(c)
                if c + 1 < NPAIR:
                    load_w(c + 1)
            for g in range(PASSES):
                turn(ip - 1, g)
                if ip == NPAIR and g == 2:
                    quantize(NPAIR - 1, 0, 2)
            for x in EXTRAS.get(ip, []):
                x[0](*x[1:])
            if ip == 3:
                for a in range(2):
                    project(0, a)
                rope_tables()
                cast(4)
                load_w(5)
            for a in range(2):
                project(ip - 2, a)
            if ip == 11:
                norm_a(0)
            if ip in (13, 14, 15, 16):
                emit_parked(0 if ip < 15 else 4, 2 * ((ip - 1) % 2), False)
                emit_parked(0 if ip < 15 else 4, 2 * ((ip - 1) % 2) + 1, False)
        quantize(NPAIR - 1, 2, 4)
        sumsq(2, 1)
        for a in range(2):
            project(NPAIR - 1, a, 0, 2)
        rope_tokens_early(24, 0, turn_y(24, 0))
        sumsq(3, 0)
        for a in range(2):
            project(NPAIR - 1, a, 2, 4)
        for a in range(2):
            leave(NH - 2 + a)
        rope_tokens_early(24, 1, turn_y(24, 1))
        sumsq(3, 1)
        sumsq(4, 0)
        sumsq(4, 1)
        norm_a(1)
        norm_b(1)
        for j in range(2):
            finish_early(24, j)
        order = [(12, 2), (12, 3), (16, 0), (24, 2), (16, 1), (24, 3), (16, 2), (28, 0), (16, 3), (28, 1), (20, 0), (28, 2), (20, 1), (28, 3), (20, 2), (20, 3)]
        banks = {}
        for i in range(len(order) + 5):
            if i < len(order):
                h0, j = order[i]
                banks[i] = turn_y(h0, j) if h0 >= 24 else back(h0, 4, j)
            if i >= 5:
                h0, j = order[i - 5]
                if h0 >= 24:
                    rope_tokens(h0, j, banks[i - 5])
                else:
                    flush(h0, 4, j, False, banks[i - 5])
